import numpy as np
import ml_dtypes


def mxq(x, axis, fmt="e4m3"):
    dtype, down = {"e4m3": (ml_dtypes.float8_e4m3fn, 7), "e5m2": (ml_dtypes.float8_e5m2, 14)}[fmt]
    v = np.moveaxis(np.asarray(x, np.float32).astype(ml_dtypes.bfloat16).astype(np.float64), axis, -1)
    blocks = v.reshape(v.shape[:-1] + (-1, 32))
    amax = np.abs(blocks).max(-1, keepdims=True)
    byte = np.maximum(np.where(amax > 0, np.frexp(amax)[1] - 1 + 127, 0) - down, 1)
    scale = np.exp2(byte - 127.0)
    codes = (blocks / scale).astype(np.float32).astype(dtype).astype(np.float64)
    return np.moveaxis((codes * scale).reshape(v.shape), -1, axis)


WIDE = False


def mx_kscale(k):
    if not WIDE:
        return np.ones(k)
    levels = np.array([18, -18])
    if k % 512:
        return np.exp2(np.random.permutation(np.resize(levels, k // 32))).repeat(32)
    a = np.empty((k // 512, 16))
    for p in range(k // 512):
        a[p, :8] = np.random.permutation(np.resize(levels, 8))
        for g in range(8):
            far = levels[np.abs(levels - a[p, g]) >= 10]
            a[p, g + 8] = far[np.random.randint(len(far))]
    return np.exp2(a.ravel()).repeat(32)


BF16 = ml_dtypes.bfloat16


def bf(x):
    return np.asarray(x, np.float32).astype(BF16)


def f64(x):
    return np.asarray(x).astype(np.float64)


B, N, K, H, NUM_IN = 8, 64, 8, 512, 512
T = B * N * K


def setup_inputs():
    s = mx_kscale(T).reshape(B, N, K)[:, :, 0]
    w = mx_kscale(H)
    v = mx_kscale(H)
    u = np.random.standard_normal((B, N, H))
    e = np.random.standard_normal((B, N, K, H))
    h1_0 = bf(np.maximum((u[:, :, None, :] + e) * 0.7, 0.0))
    h_V = bf(np.random.standard_normal((B, N, H)))
    mask = np.random.random((B, N, K)) < 0.9
    W2_0 = bf(np.random.standard_normal((H, H)) * 1.4 / np.sqrt(H))
    b2 = bf(np.random.standard_normal(H) * 0.2)
    W3_0 = bf(np.random.standard_normal((H, H)) * 2.8 / np.sqrt(H))
    b3 = bf(np.random.standard_normal(H) * 0.2)
    g = np.random.standard_normal((B, N, H)) * np.exp2(np.random.randint(-6, 1, (B, N, 1))) * 4.0
    z = f64(h1_0) @ f64(W2_0) + f64(b2)
    mask = mask & (np.min(np.abs(z), axis=-1) > 1e-5)
    return {"h1": bf(f64(h1_0) * s[:, :, None, None]),
            "h_V": h_V,
            "mask_attend": bf(mask),
            "W2": bf(f64(W2_0) / v),
            "b2": b2,
            "W3": bf(f64(W3_0) * v[:, None] / w),
            "b3": b3,
            "z": np.asarray(z, np.float32),
            "grad_out": bf(g / s[:, :, None] * w)}


def reference(h1, h_V, mask_attend, W2, b2, W3, b3, z, grad_out):
    dh = mxq(f64(grad_out).reshape(B * N, H), 1, "e5m2") @ mxq(f64(W3), 1, "e4m3").T
    f = f64(mask_attend)[..., None] / K
    dz1 = dh.reshape(B, N, 1, H) * f * (f64(z) > 0.0)
    dz1 = dz1.reshape(T, H)
    dh1 = mxq(dz1, 1, "e5m2") @ mxq(f64(W2), 1, "e4m3").T
    dW2 = mxq(f64(h1).reshape(T, H), 0, "e4m3").T @ mxq(dz1, 0, "e5m2")
    return dh1.reshape(B, N, K, H), dW2

@@ -1,0 +1,418 @@
+from contextlib import ExitStack
+
+import concourse.mybir as mybir
+from concourse.masks import make_identity
+
+F32 = mybir.dt.float32
+BF16 = mybir.dt.bfloat16
+U32 = mybir.dt.uint32
+U8 = mybir.dt.uint8
+E4M3 = mybir.dt.float8_e4m3fn_x4
+E5M2 = mybir.dt.float8_e5m2_x4
+ALU = mybir.AluOpType
+ACT = mybir.ActivationFunctionType
+
+P = 128
+H = 512
+NODES = 512
+EDGES = 4096
+GROUPS = 8
+J = 4
+TCS = (1, 2, 3, 4, 6)
+TI = 128
+CS = 2
+GS = 4
+SW = 6
+SW6 = 3
+SB = False
+QD = 4
+EV = True
+ZB = 5
+OB = 4
+BANKS = {"acc": 3, "mm": 2, "dh": 1, "trA": 1, "trB": 1}
+FMAX = (2.0 - 2.0 ** -23) * 2.0 ** 127
+
+FLOPS = 2 * H * H * (NODES + EDGES + EDGES)
+BYTES = 2 * (EDGES * H + EDGES + 2 * H * H + NODES * H) + 4 * (EDGES * H + EDGES * H + H * H)
+
+
+def tile_mpnnlayer_pb_v_kernel(tc, h1, h_V, mask_attend, W2, b2, W3, b3, z, grad_out, out_0, out_1):
+    nc = tc.nc
+    h1_v = h1.rearrange("b n k w -> (b n k) w").rearrange("(g p j) w -> p g j w", p=P, j=J)
+    z_v = z.rearrange("b n k w -> (b n k) w").rearrange("(g p j) w -> p g j w", p=P, j=J)
+    o_v = out_0.rearrange("b n k w -> (b n k) w").rearrange("(g p j) w -> p g j w", p=P, j=J)
+    mask_v = mask_attend.rearrange("b n k -> (b n k)").rearrange("(g c) -> g c", g=GROUPS)
+    grad_v = grad_out.rearrange("b n w -> (b n) w").rearrange("(t p) w -> p t w", p=P)
+    w2_v = W2.rearrange("(b r v) w -> r b v w", b=2, v=2)
+    w3_v = W3.rearrange("(b r v) w -> r b v w", b=2, v=2)
+
+    with ExitStack() as ctx:
+        ctx.enter_context(tc.manual_schedule())
+        sb = ctx.enter_context(tc.tile_pool(name="sb", bufs=1))
+        ps = ctx.enter_context(tc.psum_pool(name="ps", bufs=2))
+
+        def new(shape, dtype, tag, bufs=1):
+            return sb.tile(shape, dtype, name=tag, tag=tag, bufs=bufs, align_bytes=64)
+
+        def bank(tag):
+            return ps.tile([P, 512], F32, name=tag, tag=tag, bufs=BANKS[tag])
+
+        ident = new([P, P], F32, "ident")
+        make_identity(nc, ident[:])
+        mk = new([P, H], BF16, "mk")
+        nc.vector.memset(mk[:], 0.0)
+
+        g_raw = new([P, 4, H], BF16, "g_raw")
+        w3_raw = new([P, J, H], BF16, "w3_raw")
+        w2_raw = new([P, J, H], BF16, "w2_raw")
+
+        def load_w(raw, view, b):
+            nc.sync.dma_start(out=raw[:, 2 * b:2 * b + 2, :], in_=view[:, b])
+
+        z_t = {}
+        h1_t = {}
+
+        def load_z(g):
+            if g < GROUPS:
+                z_t[g] = new([P, J, H], F32, "z", ZB)
+                nc.sync.dma_start(out=z_t[g][:], in_=z_v[:, g])
+
+        def load_h1(g):
+            if g < GROUPS:
+                h1_t[g] = new([P, J, H], BF16, "h1", ZB)
+                nc.sync.dma_start(out=h1_t[g][:], in_=h1_v[:, g])
+
+        load_w(w3_raw, w3_v, 0)
+        load_w(w3_raw, w3_v, 1)
+        nc.sync.dma_start(out=g_raw[:, 0, :], in_=grad_v[:, 0, :])
+        nc.sync.dma_start(out=mk[0:GROUPS, :], in_=mask_v)
+        load_z(0)
+        load_h1(0)
+        load_w(w2_raw, w2_v, 0)
+        load_w(w2_raw, w2_v, 1)
+        nc.sync.dma_start(out=g_raw[:, 1:4, :], in_=grad_v[:, 1:4, :])
+        load_z(1)
+        load_h1(1)
+        for g in range(2, ZB):
+            load_z(g)
+            load_h1(g)
+
+        def transpose_words(dst, words):
+            for u in range(2):
+                nc.tensor.transpose(dst[:, u, :], words[:, u:256:2], ident[:])
+
+        def words_of(tile3, j):
+            return tile3[:, j, :].bitcast(F32)
+
+        g_codes = new([P, 2 * NODES], U32, "g_codes")
+        g_scl = new([P, 2 * NODES], U8, "g_scl")
+
+        def g_transpose(t, tag):
+            b = bank(tag)
+            bv = b[:].rearrange("p (v u r) -> p v u r", u=2, r=P)
+            transpose_words(bv[:, 0], words_of(g_raw, t))
+            return bv
+
+        def g_tile():
+            return new([P, 2 * P * 4], BF16, "gt", 4)
+
+        def g_copy(copy, gt, bv, half):
+            rows = slice(64 * half, 64 * half + 64) if half < 2 else slice(0, P)
+            n = P if half == 2 else 64
+            copy(
+                out=gt[:].bitcast(F32).rearrange("p (r d u) -> p r d u", d=2, u=2)[:, rows],
+                in_=bv[:, 0, :, rows].rearrange("p u r -> p r u").unsqueeze(2).to_broadcast([P, n, 2, 2]),
+            )
+            return gt
+
+        def g_quant(t, gt, half):
+            lo, hi = (0, 256) if half == 2 else (128 * half, 128 * half + 128)
+            nc.vector.quantize_mx(
+                out=g_codes[:, 256 * t + lo:256 * t + hi].bitcast(E5M2), scales=g_scl[:, 256 * t + lo:256 * t + hi],
+                in_=gt[:, 4 * lo:4 * hi])
+
+        def w_bank(raw, b, tag):
+            bk = bank(tag)
+            bv = bk[:].rearrange("p (v u r) -> p v u r", u=2, r=P)
+            for v in range(2):
+                transpose_words(bv[:, v], words_of(raw, 2 * b + v))
+            return bv
+
+        def w_copy(copy, dst, b, bv):
+            copy(
+                out=dst[:].bitcast(F32).rearrange("p (b r v u) -> p b r v u", b=2, v=2, u=2)[:, b],
+                in_=bv.rearrange("p v u r -> p r v u"),
+            )
+
+        def w_quant(codes, scl, dst, b):
+            cols = slice(256 * b, 256 * (b + 1))
+            nc.vector.quantize_mx(out=codes[:, cols].bitcast(E4M3), scales=scl[:, cols], in_=dst[:, 1024 * b:1024 * (b + 1)])
+
+        vcopy = nc.vector.tensor_copy
+        scopy = nc.scalar.copy
+
+        w3_t = new([P, J * H], BF16, "w3_t")
+        w3_codes = new([P, H], U32, "w3_codes")
+        w3_scl = new([P, H], U8, "w3_scl")
+        w_copy(scopy, w3_t, 0, w_bank(w3_raw, 0, "mm"))
+        w_copy(vcopy, w3_t, 1, w_bank(w3_raw, 1, "mm"))
+        gb0 = g_transpose(0, "acc")
+        gt0 = g_tile()
+        g_copy(scopy, gt0, gb0, 0)
+        mb = bank("acc")
+        mv = mb[:].rearrange("p (v u r) -> p v u r", u=2, r=P)
+        transpose_words(mv[:, 0], mk[:].bitcast(F32))
+        w_quant(w3_codes, w3_scl, w3_t, 0)
+        w_quant(w3_codes, w3_scl, w3_t, 1)
+        g_quant(0, gt0, 0)
+        m_t = new([P, GROUPS * J], BF16, "m_t")
+        vcopy(
+            out=m_t[:].bitcast(F32).rearrange("p (g u) -> p g u", u=2),
+            in_=mv[:, 0, :, 0:GROUPS].rearrange("p u g -> p g u"),
+        )
+        thr = new([P, GROUPS * J], F32, "thr")
+        nc.vector.tensor_scalar(out=thr[:], in0=m_t[:], scalar1=-FMAX, scalar2=FMAX, op0=ALU.mult, op1=ALU.add)
+
+        dh_t = {}
+
+        def dh_matmul(g):
+            if g < GROUPS:
+                dh_t[g] = bank("dh")
+                cols = slice(P * g, P * (g + 1))
+                nc.tensor.matmul_mx(
+                    out=dh_t[g][:],
+                    lhsT=g_codes[:, cols].bitcast(E5M2), lhsT_scale=g_scl[:, cols],
+                    rhs=w3_codes[:].bitcast(E4M3), rhs_scale=w3_scl[:],
+                    start=True, stop=True,
+                )
+
+        dh_matmul(0)
+        g_copy(scopy, gt0, gb0, 1)
+        gts = {}
+
+        dz_t, dzi_t, dzc_t, dzs_t, h1i_t, h1c_t, h1s_t = {}, {}, {}, {}, {}, {}, {}
+        tr_t, dzT_t, tc_t, ts_t, o_t = {}, {}, {}, {}, {}
+        w2_codes = new([P, H], U32, "w2_codes")
+        w2_scl = new([P, H], U8, "w2_scl")
+
+        def h1_interleave(g):
+            h1i_t[g] = new([P, J * H], BF16, "h1i", 1)
+            nc.gpsimd.tensor_scalar(
+                out=h1i_t[g][:].rearrange("p (w j) -> p w j", j=J), in0=h1_t[g][:].rearrange("p j w -> p w j"),
+                scalar1=1.0, scalar2=0.0, op0=ALU.mult, op1=ALU.add)
+
+        def h1_quant(g):
+            h1c_t[g] = new([P, H], U32, "h1c", 8)
+            h1s_t[g] = new([P, H], U8, "h1s", 8)
+            nc.vector.quantize_mx(out=h1c_t[g][:].bitcast(E4M3), scales=h1s_t[g][:], in_=h1i_t[g][:])
+
+        def dz_compute(g, j):
+            if j == 0:
+                dz_t[g] = new([P, J, H], BF16, "dz", 3)
+            nc.vector.scalar_tensor_tensor(
+                out=dz_t[g][:, j, :], in0=z_t[g][:, j, :], scalar=thr[:, J * g + j:J * g + j + 1],
+                in1=dh_t[g][:], op0=ALU.is_gt, op1=ALU.mult,
+            )
+
+        def dz_interleave(copy, g, lo, hi):
+            if hi == lo:
+                return
+            if g not in dzi_t:
+                dzi_t[g] = new([P, J * H], BF16, "dzi", 2)
+            out = dzi_t[g][:].rearrange("p (w j) -> p w j", j=J)[:, lo:hi, :]
+            in_ = dz_t[g][:].rearrange("p j w -> p w j")[:, lo:hi, :]
+            copy(
+                out=out.rearrange("p (c i) j -> p c j i", i=4),
+                in_=in_.rearrange("p (c i) j -> p c j i", i=4),
+            )
+
+        def dz_quant(g):
+            dzc_t[g] = new([P, H], U32, "dzc", 8)
+            dzs_t[g] = new([P, H], U8, "dzs", 8)
+            nc.vector.quantize_mx(out=dzc_t[g][:].bitcast(E5M2), scales=dzs_t[g][:], in_=dzi_t[g][:])
+
+        def dzT_transpose(g, h):
+            bk = bank("trB" if h == 1 and g < GROUPS - 2 else "trA")
+            tr_t[g, h] = bk[:].rearrange("p (v u r) -> p v u r", u=2, r=P)
+            for v in range(2):
+                transpose_words(tr_t[g, h][:, v], words_of(dz_t[g], 2 * h + v))
+
+        def dzT_copy(g, h):
+            dzT_t[g, h] = new([P, 2 * P * 4], BF16, "dzT", 3)
+            (scopy if h == 1 and g in TCS else vcopy)(
+                out=dzT_t[g, h][:].bitcast(F32).rearrange("p (v r u) -> p v r u", r=P, u=2),
+                in_=tr_t[g, h].rearrange("p v u r -> p v r u"),
+            )
+
+        def dzT_quant(g, h):
+            tc_t[g, h] = new([P, 2 * P], U32, "tcod", 3)
+            ts_t[g, h] = new([P, 2 * P], U8, "tscl", 3)
+            nc.vector.quantize_mx(out=tc_t[g, h][:].bitcast(E5M2), scales=ts_t[g, h][:], in_=dzT_t[g, h][:])
+
+        def out0_matmul(g, h, v):
+            bk = bank("mm")
+            cols = slice(P * v, P * (v + 1))
+            nc.tensor.matmul_mx(
+                out=bk[:],
+                lhsT=tc_t[g, h][:, cols].bitcast(E5M2), lhsT_scale=ts_t[g, h][:, cols],
+                rhs=w2_codes[:].bitcast(E4M3), rhs_scale=w2_scl[:],
+                start=True, stop=True,
+            )
+            return bk
+
+        def out0_copy_s(g, h, v, bk):
+            nc.scalar.activation(out=o_t[g][:, 2 * h + v, :], in_=bk[:], func=ACT.Copy, scale=0.125)
+
+        def out0_copy_v(g, h, v, bk):
+            nc.vector.tensor_scalar(out=o_t[g][:, 2 * h + v, :], in0=bk[:], scalar1=0.125, scalar2=None, op0=ALU.mult)
+
+        def out0_half(g, h, emits=None):
+            if h == 0:
+                o_t[g] = new([P, J, H], F32, "o", OB)
+            banks = [out0_matmul(g, h, v) for v in range(2)]
+            for v in range(2):
+                (out0_copy_s if emits is None else emits[v])(g, h, v, banks[v])
+
+        acc = {}
+
+        def out1_pass(g, m):
+            if g == 0:
+                acc[m] = bank("acc" if m < 3 else "trB")
+            cols = slice(P * m, P * (m + 1))
+            nc.tensor.matmul_mx(
+                out=acc[m][:],
+                lhsT=h1c_t[g][:, cols].bitcast(E4M3), lhsT_scale=h1s_t[g][:, cols],
+                rhs=dzc_t[g][:].bitcast(E5M2), rhs_scale=dzs_t[g][:],
+                start=(g == 0), stop=(g == GROUPS - 1),
+            )
+
+        last = GROUPS - 1
+        c0 = 256
+
+        def store(g, lo, hi):
+            nc.sync.dma_start(out=o_v[:, g, lo:hi], in_=o_t[g][:, lo:hi, :])
+
+        w2_t = new([P, J * H], BF16, "w2_t")
+        h1_interleave(0)
+        dz_compute(0, 0)
+        dz_compute(0, 1)
+        dzT_transpose(0, 0)
+        w_copy(scopy, w2_t, 0, w_bank(w2_raw, 0, "mm"))
+        dz_compute(0, 2)
+        dz_compute(0, 3)
+        w_copy(scopy, w2_t, 1, w_bank(w2_raw, 1, "mm"))
+        dz_interleave(scopy, 0, 0, 256)
+        g_quant(0, gt0, 1)
+        dh_matmul(1)
+        dzT_transpose(0, 1)
+        h1_quant(0)
+        dzT_copy(0, 0)
+        load_z(ZB)
+        load_h1(ZB)
+        for b in range(2):
+            w_quant(w2_codes, w2_scl, w2_t, b)
+        dzT_quant(0, 0)
+        gts[1] = g_copy(scopy, g_tile(), g_transpose(1, "acc"), 2)
+        out0_half(0, 0)
+        dzT_copy(0, 1)
+        g_quant(1, gts[1], 2)
+        dzT_quant(0, 1)
+        dz_interleave(scopy, 0, 256, H)
+        for t in (2, 3):
+            gts[t] = g_copy(scopy, g_tile(), g_transpose(t, "acc"), 2)
+        out0_half(0, 1)
+        store(0, 0, J)
+
+        for g in range(1, last):
+            h1_interleave(g)
+            if g > 1 and g - 1 not in TCS:
+                dzT_copy(g - 1, 1)
+            dz_compute(g, 0)
+            dz_compute(g, 1)
+            dzT_transpose(g, 0)
+            if g > 1:
+                if g > 2:
+                    out0_half(g - 1, 0)
+                for m in range(2):
+                    out1_pass(g - 2, m)
+            dz_compute(g, 2)
+            dz_compute(g, 3)
+            dzT_copy(g, 0)
+            dh_matmul(g + 1)
+            dzT_transpose(g, 1)
+            dz_interleave(scopy, g, 0, 256)
+            if g in TCS:
+                dzT_copy(g, 1)
+            load_z(g + ZB)
+            load_h1(g + ZB)
+            if g > 1:
+                dzT_quant(g - 1, 1)
+                out0_half(g - 1, 1)
+                store(g - 1, 0, J)
+                out1_pass(g - 2, 2)
+            if g == last - 1:
+                for k in range(SW6):
+                    out1_pass(k, 3)
+            dz_interleave(scopy, g, 256, H)
+            dz_quant(g - 1)
+            dzT_quant(g, 0)
+            h1_quant(g)
+            if g == 1:
+                for t in (2, 3):
+                    g_quant(t, gts[t], 2)
+                out0_half(1, 0)
+
+        g = last
+        h1_interleave(g)
+        if g - 1 not in TCS:
+            dzT_copy(g - 1, 1)
+        dz_compute(g, 0)
+        dz_compute(g, 1)
+        dzT_transpose(g, 0)
+        out0_half(g - 1, 0)
+        store(g - 1, 0, 2)
+        for m in range(3):
+            out1_pass(g - 2, m)
+        if SB:
+            for k in range(SW6, SW):
+                out1_pass(k, 3)
+        dz_compute(g, 2)
+        dz_compute(g, 3)
+        dzT_copy(g, 0)
+        dzT_transpose(g, 1)
+        dzT_quant(g - 1, 1)
+        out0_half(g - 1, 1)
+        store(g - 1, 2, J)
+        dzT_quant(g, 0)
+        if not SB:
+            for k in range(SW6, SW):
+                out1_pass(k, 3)
+        dz_interleave(scopy, g, 0, TI)
+        dzT_copy(g, 1)
+        out0_half(g, 0)
+        store(g, 0, 1)
+        store(g, 1, 2)
+        for k in range(SW, g - 1):
+            out1_pass(k, 3)
+        dz_quant(g - 1)
+        dzT_quant(g, 1)
+        for m in range(QD):
+            out1_pass(g - 1, m)
+        h1_quant(g)
+        dz_interleave(vcopy, g, TI, H)
+        dz_quant(g)
+        out0_half(g, 1, emits=(out0_copy_s, out0_copy_v) if EV else None)
+        store(g, 2, 3)
+        store(g, 3, 4)
+        for m in range(QD, 4):
+            out1_pass(g - 1, m)
+        o1 = new([P, 4, H], F32, "o", OB)
+        o1_v = out_1.rearrange("(m p) w -> p m w", p=P)
+        for m in range(4):
+            out1_pass(g, m)
+        for m in range(4):
+            if m % 2 == 0:
+                nc.scalar.activation(out=o1[:, m, :], in_=acc[m][:], func=ACT.Copy, scale=0.125)
+            else:
+                nc.vector.tensor_scalar(out=o1[:, m, :], in0=acc[m][:], scalar1=0.125, scalar2=None, op0=ALU.mult)
+            nc.sync.dma_start(out=o1_v[:, m], in_=o1[:, m, :])

@@ -18,18 +18,11 @@ NODES = 512
 EDGES = 4096
 GROUPS = 8
 J = 4
-TCS = (1, 2, 3, 4, 6)
-TI = 128
-CS = 2
-GS = 4
-SW = 6
-SW6 = 3
-SB = False
-QD = 4
-EV = True
-ZB = 5
-OB = 4
-BANKS = {"acc": 3, "mm": 2, "dh": 1, "trA": 1, "trB": 1}
+V_COLS = 64
+S_MID = 224
+TAIL_V_COLS = 384
+STREAM_BUFS = 11
+BANKS = {"acc": 4, "ring": 3, "dh": 1}
 FMAX = (2.0 - 2.0 ** -23) * 2.0 ** 127
 
 FLOPS = 2 * H * H * (NODES + EDGES + EDGES)
@@ -38,13 +31,14 @@ BYTES = 2 * (EDGES * H + EDGES + 2 * H * H + NODES * H) + 4 * (EDGES * H + EDGES
 
 def tile_mpnnlayer_pb_v_kernel(tc, h1, h_V, mask_attend, W2, b2, W3, b3, z, grad_out, out_0, out_1):
     nc = tc.nc
-    h1_v = h1.rearrange("b n k w -> (b n k) w").rearrange("(g p j) w -> p g j w", p=P, j=J)
-    z_v = z.rearrange("b n k w -> (b n k) w").rearrange("(g p j) w -> p g j w", p=P, j=J)
-    o_v = out_0.rearrange("b n k w -> (b n k) w").rearrange("(g p j) w -> p g j w", p=P, j=J)
+    h1_v = h1.rearrange("b n k w -> (b n k) w").rearrange("(g p j) w -> p g (j w)", p=P, j=J)
+    z_v = z.rearrange("b n k w -> (b n k) w").rearrange("(g p j) w -> p g (j w)", p=P, j=J)
+    o_v = out_0.rearrange("b n k w -> (b n k) w").rearrange("(g p j) w -> p g (j w)", p=P, j=J)
     mask_v = mask_attend.rearrange("b n k -> (b n k)").rearrange("(g c) -> g c", g=GROUPS)
     grad_v = grad_out.rearrange("b n w -> (b n) w").rearrange("(t p) w -> p t w", p=P)
-    w2_v = W2.rearrange("(b r v) w -> r b v w", b=2, v=2)
-    w3_v = W3.rearrange("(b r v) w -> r b v w", b=2, v=2)
+    w2_v = W2.rearrange("(b r v) w -> r b (v w)", b=2, v=2)
+    w3_v = W3.rearrange("(b r v) w -> r b (v w)", b=2, v=2)
+    o1_v = out_1.rearrange("(m p) w -> p m w", p=P)
 
     with ExitStack() as ctx:
         ctx.enter_context(tc.manual_schedule())
@@ -57,189 +51,175 @@ def tile_mpnnlayer_pb_v_kernel(tc, h1, h_V, mask_attend, W2, b2, W3, b3, z, grad
         def bank(tag):
             return ps.tile([P, 512], F32, name=tag, tag=tag, bufs=BANKS[tag])
 
+        def blocks(bk):
+            return bk[:].rearrange("p (v u r) -> p v u r", u=2, r=P)
+
+        vcopy = nc.vector.tensor_copy
+        scopy = nc.scalar.copy
+
         ident = new([P, P], F32, "ident")
         make_identity(nc, ident[:])
         mk = new([P, H], BF16, "mk")
         nc.vector.memset(mk[:], 0.0)
 
-        g_raw = new([P, 4, H], BF16, "g_raw")
-        w3_raw = new([P, J, H], BF16, "w3_raw")
-        w2_raw = new([P, J, H], BF16, "w2_raw")
+        def load(view, width, dtype, tag, bufs):
+            t = new([P, width], dtype, tag, bufs)
+            nc.sync.dma_start(out=t[:], in_=view)
+            return t
 
-        def load_w(raw, view, b):
-            nc.sync.dma_start(out=raw[:, 2 * b:2 * b + 2, :], in_=view[:, b])
+        z_t, h1_t = {}, {}
 
-        z_t = {}
-        h1_t = {}
+        def load_group(g):
+            z_t[g] = new([P, J * H], F32, "stream", STREAM_BUFS)
+            nc.sync.dma_start(out=z_t[g][:, 0:2 * H], in_=z_v[:, g, 0:2 * H])
+            h1_t[g] = load(h1_v[:, g], J * H, BF16, "h1", GROUPS)
+            nc.sync.dma_start(out=z_t[g][:, 2 * H:J * H], in_=z_v[:, g, 2 * H:J * H])
 
-        def load_z(g):
-            if g < GROUPS:
-                z_t[g] = new([P, J, H], F32, "z", ZB)
-                nc.sync.dma_start(out=z_t[g][:], in_=z_v[:, g])
-
-        def load_h1(g):
-            if g < GROUPS:
-                h1_t[g] = new([P, J, H], BF16, "h1", ZB)
-                nc.sync.dma_start(out=h1_t[g][:], in_=h1_v[:, g])
-
-        load_w(w3_raw, w3_v, 0)
-        load_w(w3_raw, w3_v, 1)
-        nc.sync.dma_start(out=g_raw[:, 0, :], in_=grad_v[:, 0, :])
+        w3_raw, w2_raw, g_raw = {}, {}, {}
+        w3_raw[0] = load(w3_v[:, 0], 2 * H, BF16, "w_raw", 4)
+        g_raw[0] = load(grad_v[:, 0], H, BF16, "g_raw", 4)
+        w3_raw[1] = load(w3_v[:, 1], 2 * H, BF16, "w_raw", 4)
         nc.sync.dma_start(out=mk[0:GROUPS, :], in_=mask_v)
-        load_z(0)
-        load_h1(0)
-        load_w(w2_raw, w2_v, 0)
-        load_w(w2_raw, w2_v, 1)
-        nc.sync.dma_start(out=g_raw[:, 1:4, :], in_=grad_v[:, 1:4, :])
-        load_z(1)
-        load_h1(1)
-        for g in range(2, ZB):
-            load_z(g)
-            load_h1(g)
+        load_group(0)
+        for b in range(2):
+            w2_raw[b] = load(w2_v[:, b], 2 * H, BF16, "w_raw", 4)
+        g_raw[1] = load(grad_v[:, 1], H, BF16, "g_raw", 4)
+        load_group(1)
+        for t in (2, 3):
+            g_raw[t] = load(grad_v[:, t], H, BF16, "g_raw", 4)
+        for g in range(2, GROUPS):
+            load_group(g)
 
-        def transpose_words(dst, words):
+        def transpose_stepped(dst, words):
             for u in range(2):
                 nc.tensor.transpose(dst[:, u, :], words[:, u:256:2], ident[:])
 
-        def words_of(tile3, j):
-            return tile3[:, j, :].bitcast(F32)
+        def transpose_sorted(dst, words):
+            for u in range(2):
+                nc.tensor.transpose(dst[:, u, :], words[:, P * u:P * (u + 1)], ident[:])
 
         g_codes = new([P, 2 * NODES], U32, "g_codes")
         g_scl = new([P, 2 * NODES], U8, "g_scl")
+        g_wide = {}
 
-        def g_transpose(t, tag):
-            b = bank(tag)
-            bv = b[:].rearrange("p (v u r) -> p v u r", u=2, r=P)
-            transpose_words(bv[:, 0], words_of(g_raw, t))
-            return bv
-
-        def g_tile():
-            return new([P, 2 * P * 4], BF16, "gt", 4)
-
-        def g_copy(copy, gt, bv, half):
-            rows = slice(64 * half, 64 * half + 64) if half < 2 else slice(0, P)
-            n = P if half == 2 else 64
-            copy(
-                out=gt[:].bitcast(F32).rearrange("p (r d u) -> p r d u", d=2, u=2)[:, rows],
-                in_=bv[:, 0, :, rows].rearrange("p u r -> p r u").unsqueeze(2).to_broadcast([P, n, 2, 2]),
+        def g_copy(t, bv, lo, hi):
+            if t not in g_wide:
+                g_wide[t] = new([P, 2 * P * 4], BF16, "g_wide", 3)
+            scopy(
+                out=g_wide[t][:].bitcast(F32).rearrange("p (r d u) -> p r d u", d=2, u=2)[:, lo:hi],
+                in_=bv[:, :, lo:hi].rearrange("p u r -> p r u").unsqueeze(2).to_broadcast([P, hi - lo, 2, 2]),
             )
-            return gt
 
-        def g_quant(t, gt, half):
-            lo, hi = (0, 256) if half == 2 else (128 * half, 128 * half + 128)
-            nc.vector.quantize_mx(
-                out=g_codes[:, 256 * t + lo:256 * t + hi].bitcast(E5M2), scales=g_scl[:, 256 * t + lo:256 * t + hi],
-                in_=gt[:, 4 * lo:4 * hi])
+        def g_quant(t, lo, hi):
+            cols = slice(256 * t + 2 * lo, 256 * t + 2 * hi)
+            nc.vector.quantize_mx(out=g_codes[:, cols].bitcast(E5M2), scales=g_scl[:, cols], in_=g_wide[t][:, 8 * lo:8 * hi])
 
-        def w_bank(raw, b, tag):
-            bk = bank(tag)
-            bv = bk[:].rearrange("p (v u r) -> p v u r", u=2, r=P)
+        def w_bank(transposer, raw, tag):
+            bv = blocks(bank(tag))
             for v in range(2):
-                transpose_words(bv[:, v], words_of(raw, 2 * b + v))
+                transposer(bv[:, v], raw[:].bitcast(F32)[:, 256 * v:256 * (v + 1)])
             return bv
 
-        def w_copy(copy, dst, b, bv):
-            copy(
-                out=dst[:].bitcast(F32).rearrange("p (b r v u) -> p b r v u", b=2, v=2, u=2)[:, b],
-                in_=bv.rearrange("p v u r -> p r v u"),
-            )
+        def w_copy(copy, bv):
+            dst = new([P, 2 * H], BF16, "w_t", 2)
+            copy(out=dst[:].bitcast(F32).rearrange("p (r v u) -> p r v u", v=2, u=2), in_=bv.rearrange("p v u r -> p r v u"))
+            return dst
 
-        def w_quant(codes, scl, dst, b):
+        def w_quant(codes, scl, b, src):
             cols = slice(256 * b, 256 * (b + 1))
-            nc.vector.quantize_mx(out=codes[:, cols].bitcast(E4M3), scales=scl[:, cols], in_=dst[:, 1024 * b:1024 * (b + 1)])
+            nc.vector.quantize_mx(out=codes[:, cols].bitcast(E4M3), scales=scl[:, cols], in_=src[:])
 
-        vcopy = nc.vector.tensor_copy
-        scopy = nc.scalar.copy
+        def w2_sort(b):
+            dst = new([P, 2 * H], BF16, "w2_sorted", 2)
+            scopy(
+                out=dst[:].rearrange("p (v u q i) -> p v u q i", v=2, u=2, i=16),
+                in_=w2_raw[b][:].rearrange("p (v q u i) -> p v u q i", v=2, u=2, i=16),
+            )
+            return dst
 
-        w3_t = new([P, J * H], BF16, "w3_t")
         w3_codes = new([P, H], U32, "w3_codes")
         w3_scl = new([P, H], U8, "w3_scl")
-        w_copy(scopy, w3_t, 0, w_bank(w3_raw, 0, "mm"))
-        w_copy(vcopy, w3_t, 1, w_bank(w3_raw, 1, "mm"))
-        gb0 = g_transpose(0, "acc")
-        gt0 = g_tile()
-        g_copy(scopy, gt0, gb0, 0)
-        mb = bank("acc")
-        mv = mb[:].rearrange("p (v u r) -> p v u r", u=2, r=P)
-        transpose_words(mv[:, 0], mk[:].bitcast(F32))
-        w_quant(w3_codes, w3_scl, w3_t, 0)
-        w_quant(w3_codes, w3_scl, w3_t, 1)
-        g_quant(0, gt0, 0)
+        w2_codes = new([P, H], U32, "w2_codes")
+        w2_scl = new([P, H], U8, "w2_scl")
+        w3a = w_copy(vcopy, w_bank(transpose_stepped, w3_raw[0], "ring"))
+        gb0 = blocks(bank("acc"))[:, 0]
+        transpose_stepped(gb0, g_raw[0][:].bitcast(F32))
+        g_copy(0, gb0, 0, 64)
+        w3b = w_copy(scopy, w_bank(transpose_stepped, w3_raw[1], "ring"))
+        mv = blocks(bank("acc"))[:, 0]
+        transpose_stepped(mv, mk[:].bitcast(F32))
+        w_quant(w3_codes, w3_scl, 0, w3a)
+        g_quant(0, 0, 64)
         m_t = new([P, GROUPS * J], BF16, "m_t")
-        vcopy(
-            out=m_t[:].bitcast(F32).rearrange("p (g u) -> p g u", u=2),
-            in_=mv[:, 0, :, 0:GROUPS].rearrange("p u g -> p g u"),
-        )
+        vcopy(out=m_t[:].bitcast(F32).rearrange("p (g u) -> p g u", u=2), in_=mv[:, :, 0:GROUPS].rearrange("p u g -> p g u"))
+        w_quant(w3_codes, w3_scl, 1, w3b)
         thr = new([P, GROUPS * J], F32, "thr")
         nc.vector.tensor_scalar(out=thr[:], in0=m_t[:], scalar1=-FMAX, scalar2=FMAX, op0=ALU.mult, op1=ALU.add)
 
         dh_t = {}
 
         def dh_matmul(g):
-            if g < GROUPS:
-                dh_t[g] = bank("dh")
-                cols = slice(P * g, P * (g + 1))
-                nc.tensor.matmul_mx(
-                    out=dh_t[g][:],
-                    lhsT=g_codes[:, cols].bitcast(E5M2), lhsT_scale=g_scl[:, cols],
-                    rhs=w3_codes[:].bitcast(E4M3), rhs_scale=w3_scl[:],
-                    start=True, stop=True,
-                )
+            dh_t[g] = bank("dh")
+            cols = slice(P * g, P * (g + 1))
+            nc.tensor.matmul_mx(
+                out=dh_t[g][:],
+                lhsT=g_codes[:, cols].bitcast(E5M2), lhsT_scale=g_scl[:, cols],
+                rhs=w3_codes[:].bitcast(E4M3), rhs_scale=w3_scl[:],
+                start=True, stop=True,
+            )
 
         dh_matmul(0)
-        g_copy(scopy, gt0, gb0, 1)
-        gts = {}
+        g_copy(0, gb0, 64, P)
+        g_quant(0, 64, P)
 
         dz_t, dzi_t, dzc_t, dzs_t, h1i_t, h1c_t, h1s_t = {}, {}, {}, {}, {}, {}, {}
-        tr_t, dzT_t, tc_t, ts_t, o_t = {}, {}, {}, {}, {}
-        w2_codes = new([P, H], U32, "w2_codes")
-        w2_scl = new([P, H], U8, "w2_scl")
+        tr_t, dzT_t, tc_t, ts_t, o_t, mm_t, acc = {}, {}, {}, {}, {}, {}, {}
 
         def h1_interleave(g):
             h1i_t[g] = new([P, J * H], BF16, "h1i", 1)
             nc.gpsimd.tensor_scalar(
-                out=h1i_t[g][:].rearrange("p (w j) -> p w j", j=J), in0=h1_t[g][:].rearrange("p j w -> p w j"),
+                out=h1i_t[g][:].rearrange("p (w j) -> p w j", j=J), in0=h1_t[g][:].rearrange("p (j w) -> p w j", j=J),
                 scalar1=1.0, scalar2=0.0, op0=ALU.mult, op1=ALU.add)
 
         def h1_quant(g):
-            h1c_t[g] = new([P, H], U32, "h1c", 8)
-            h1s_t[g] = new([P, H], U8, "h1s", 8)
+            h1c_t[g] = new([P, H], U32, "h1c", 3)
+            h1s_t[g] = new([P, H], U8, "h1s", 3)
             nc.vector.quantize_mx(out=h1c_t[g][:].bitcast(E4M3), scales=h1s_t[g][:], in_=h1i_t[g][:])
 
-        def dz_compute(g, j):
-            if j == 0:
-                dz_t[g] = new([P, J, H], BF16, "dz", 3)
-            nc.vector.scalar_tensor_tensor(
-                out=dz_t[g][:, j, :], in0=z_t[g][:, j, :], scalar=thr[:, J * g + j:J * g + j + 1],
-                in1=dh_t[g][:], op0=ALU.is_gt, op1=ALU.mult,
-            )
+        def dz_compute(g, h):
+            if h == 0:
+                dz_t[g] = new([P, J * H], BF16, "dz", 3)
+            for j in (2 * h, 2 * h + 1):
+                for u in range(2):
+                    nc.vector.scalar_tensor_tensor(
+                        out=dz_t[g][:, H * j + 256 * u:H * j + 256 * (u + 1)].rearrange("p (q i) -> p q i", i=16),
+                        in0=z_t[g][:, H * j:H * (j + 1)].rearrange("p (q u i) -> p q u i", u=2, i=16)[:, :, u, :],
+                        scalar=thr[:, J * g + j:J * g + j + 1],
+                        in1=dh_t[g][:].rearrange("p (q u i) -> p q u i", u=2, i=16)[:, :, u, :],
+                        op0=ALU.is_gt, op1=ALU.mult,
+                    )
 
         def dz_interleave(copy, g, lo, hi):
-            if hi == lo:
-                return
             if g not in dzi_t:
                 dzi_t[g] = new([P, J * H], BF16, "dzi", 2)
             out = dzi_t[g][:].rearrange("p (w j) -> p w j", j=J)[:, lo:hi, :]
-            in_ = dz_t[g][:].rearrange("p j w -> p w j")[:, lo:hi, :]
-            copy(
-                out=out.rearrange("p (c i) j -> p c j i", i=4),
-                in_=in_.rearrange("p (c i) j -> p c j i", i=4),
-            )
+            in_ = dz_t[g][:].rearrange("p (j w) -> p w j", j=J)[:, lo:hi, :]
+            copy(out=out.rearrange("p (c i) j -> p c j i", i=4), in_=in_.rearrange("p (c i) j -> p c j i", i=4))
 
         def dz_quant(g):
-            dzc_t[g] = new([P, H], U32, "dzc", 8)
-            dzs_t[g] = new([P, H], U8, "dzs", 8)
+            dzc_t[g] = new([P, H], U32, "dzc", 3)
+            dzs_t[g] = new([P, H], U8, "dzs", 3)
             nc.vector.quantize_mx(out=dzc_t[g][:].bitcast(E5M2), scales=dzs_t[g][:], in_=dzi_t[g][:])
 
         def dzT_transpose(g, h):
-            bk = bank("trB" if h == 1 and g < GROUPS - 2 else "trA")
-            tr_t[g, h] = bk[:].rearrange("p (v u r) -> p v u r", u=2, r=P)
+            tr_t[g, h] = blocks(bank("ring"))
             for v in range(2):
-                transpose_words(tr_t[g, h][:, v], words_of(dz_t[g], 2 * h + v))
+                j = 2 * h + v
+                transpose_sorted(tr_t[g, h][:, v], dz_t[g][:].bitcast(F32)[:, 256 * j:256 * (j + 1)])
 
-        def dzT_copy(g, h):
+        def dzT_copy(copy, g, h):
             dzT_t[g, h] = new([P, 2 * P * 4], BF16, "dzT", 3)
-            (scopy if h == 1 and g in TCS else vcopy)(
+            copy(
                 out=dzT_t[g, h][:].bitcast(F32).rearrange("p (v r u) -> p v r u", r=P, u=2),
                 in_=tr_t[g, h].rearrange("p v u r -> p v r u"),
             )
@@ -249,35 +229,33 @@ def tile_mpnnlayer_pb_v_kernel(tc, h1, h_V, mask_attend, W2, b2, W3, b3, z, grad
             ts_t[g, h] = new([P, 2 * P], U8, "tscl", 3)
             nc.vector.quantize_mx(out=tc_t[g, h][:].bitcast(E5M2), scales=ts_t[g, h][:], in_=dzT_t[g, h][:])
 
-        def out0_matmul(g, h, v):
-            bk = bank("mm")
+        def out0_matmul(g, j):
+            if j == 0:
+                o_t[g] = new([P, J * H], F32, "stream", STREAM_BUFS)
+            mm_t[g, j] = bank("ring")
+            h, v = divmod(j, 2)
             cols = slice(P * v, P * (v + 1))
             nc.tensor.matmul_mx(
-                out=bk[:],
+                out=mm_t[g, j][:],
                 lhsT=tc_t[g, h][:, cols].bitcast(E5M2), lhsT_scale=ts_t[g, h][:, cols],
                 rhs=w2_codes[:].bitcast(E4M3), rhs_scale=w2_scl[:],
                 start=True, stop=True,
             )
-            return bk
 
-        def out0_copy_s(g, h, v, bk):
-            nc.scalar.activation(out=o_t[g][:, 2 * h + v, :], in_=bk[:], func=ACT.Copy, scale=0.125)
+        def s_scale(out, in_):
+            nc.scalar.activation(out=out, in_=in_, func=ACT.Copy, scale=0.125)
 
-        def out0_copy_v(g, h, v, bk):
-            nc.vector.tensor_scalar(out=o_t[g][:, 2 * h + v, :], in0=bk[:], scalar1=0.125, scalar2=None, op0=ALU.mult)
+        def v_scale(out, in_):
+            nc.vector.tensor_scalar(out=out, in0=in_, scalar1=0.125, scalar2=None, op0=ALU.mult)
 
-        def out0_half(g, h, emits=None):
-            if h == 0:
-                o_t[g] = new([P, J, H], F32, "o", OB)
-            banks = [out0_matmul(g, h, v) for v in range(2)]
-            for v in range(2):
-                (out0_copy_s if emits is None else emits[v])(g, h, v, banks[v])
-
-        acc = {}
+        def out0_copy(scale, g, j):
+            scale(o_t[g][:, H * j:H * (j + 1)], mm_t[g, j][:])
 
         def out1_pass(g, m):
+            if g < 0:
+                return
             if g == 0:
-                acc[m] = bank("acc" if m < 3 else "trB")
+                acc[m] = bank("acc")
             cols = slice(P * m, P * (m + 1))
             nc.tensor.matmul_mx(
                 out=acc[m][:],
@@ -286,133 +264,119 @@ def tile_mpnnlayer_pb_v_kernel(tc, h1, h_V, mask_attend, W2, b2, W3, b3, z, grad
                 start=(g == 0), stop=(g == GROUPS - 1),
             )
 
-        last = GROUPS - 1
-        c0 = 256
-
         def store(g, lo, hi):
-            nc.sync.dma_start(out=o_v[:, g, lo:hi], in_=o_t[g][:, lo:hi, :])
+            nc.sync.dma_start(out=o_v[:, g, H * lo:H * hi], in_=o_t[g][:, H * lo:H * hi])
 
-        w2_t = new([P, J * H], BF16, "w2_t")
+        last = GROUPS - 1
+
         h1_interleave(0)
         dz_compute(0, 0)
-        dz_compute(0, 1)
         dzT_transpose(0, 0)
-        w_copy(scopy, w2_t, 0, w_bank(w2_raw, 0, "mm"))
-        dz_compute(0, 2)
-        dz_compute(0, 3)
-        w_copy(scopy, w2_t, 1, w_bank(w2_raw, 1, "mm"))
-        dz_interleave(scopy, 0, 0, 256)
-        g_quant(0, gt0, 1)
-        dh_matmul(1)
+        w2_sorted = [w2_sort(b) for b in range(2)]
+        w2a_bank = w_bank(transpose_sorted, w2_sorted[0], "acc")
+        dz_compute(0, 1)
         dzT_transpose(0, 1)
-        h1_quant(0)
-        dzT_copy(0, 0)
-        load_z(ZB)
-        load_h1(ZB)
-        for b in range(2):
-            w_quant(w2_codes, w2_scl, w2_t, b)
+        w2b_bank = w_bank(transpose_sorted, w2_sorted[1], "acc")
+        dh_matmul(1)
+        gb1 = blocks(bank("acc"))[:, 0]
+        transpose_stepped(gb1, g_raw[1][:].bitcast(F32))
+        dzT_copy(vcopy, 0, 0)
+        w2a = w_copy(scopy, w2a_bank)
+        w2b = w_copy(scopy, w2b_bank)
+        dz_interleave(vcopy, 0, 0, S_MID)
         dzT_quant(0, 0)
-        gts[1] = g_copy(scopy, g_tile(), g_transpose(1, "acc"), 2)
-        out0_half(0, 0)
-        dzT_copy(0, 1)
-        g_quant(1, gts[1], 2)
-        dzT_quant(0, 1)
-        dz_interleave(scopy, 0, 256, H)
-        for t in (2, 3):
-            gts[t] = g_copy(scopy, g_tile(), g_transpose(t, "acc"), 2)
-        out0_half(0, 1)
-        store(0, 0, J)
+        w_quant(w2_codes, w2_scl, 0, w2a)
+        dzT_copy(scopy, 0, 1)
+        w_quant(w2_codes, w2_scl, 1, w2b)
+        h1_quant(0)
+        g_copy(1, gb1, 0, P)
+        out0_matmul(0, 0)
+        out0_matmul(0, 1)
+        out0_copy(s_scale, 0, 0)
+        out0_copy(s_scale, 0, 1)
+        dz_interleave(scopy, 0, S_MID, H)
 
         for g in range(1, last):
             h1_interleave(g)
-            if g > 1 and g - 1 not in TCS:
-                dzT_copy(g - 1, 1)
             dz_compute(g, 0)
-            dz_compute(g, 1)
             dzT_transpose(g, 0)
-            if g > 1:
-                if g > 2:
-                    out0_half(g - 1, 0)
-                for m in range(2):
-                    out1_pass(g - 2, m)
-            dz_compute(g, 2)
-            dz_compute(g, 3)
-            dzT_copy(g, 0)
-            dh_matmul(g + 1)
+            out1_pass(g - 2, 2)
+            out1_pass(g - 2, 3)
+            dz_compute(g, 1)
             dzT_transpose(g, 1)
-            dz_interleave(scopy, g, 0, 256)
-            if g in TCS:
-                dzT_copy(g, 1)
-            load_z(g + ZB)
-            load_h1(g + ZB)
-            if g > 1:
-                dzT_quant(g - 1, 1)
-                out0_half(g - 1, 1)
-                store(g - 1, 0, J)
-                out1_pass(g - 2, 2)
-            if g == last - 1:
-                for k in range(SW6):
-                    out1_pass(k, 3)
-            dz_interleave(scopy, g, 256, H)
-            dz_quant(g - 1)
-            dzT_quant(g, 0)
-            h1_quant(g)
             if g == 1:
-                for t in (2, 3):
-                    g_quant(t, gts[t], 2)
-                out0_half(1, 0)
+                gb23 = blocks(bank("acc"))
+                for v in range(2):
+                    transpose_stepped(gb23[:, v], g_raw[2 + v][:].bitcast(F32))
+            dzT_copy(vcopy, g, 0)
+            if g <= 3:
+                g_quant(g, 0, P)
+            dh_matmul(g + 1)
+            dzT_copy(scopy, g, 1)
+            dzT_quant(g - 1, 1)
+            out0_matmul(g - 1, 2)
+            out0_matmul(g - 1, 3)
+            dz_interleave(vcopy, g, 0, V_COLS)
+            dz_interleave(scopy, g, V_COLS, S_MID)
+            dzT_quant(g, 0)
+            out0_copy(s_scale, g - 1, 2)
+            out0_copy(s_scale, g - 1, 3)
+            store(g - 1, 0, J)
+            out0_matmul(g, 0)
+            dz_quant(g - 1)
+            out1_pass(g - 1, 0)
+            out0_matmul(g, 1)
+            out1_pass(g - 1, 1)
+            h1_quant(g)
+            out0_copy(s_scale, g, 0)
+            out0_copy(s_scale, g, 1)
+            if g == 1:
+                for v in range(2):
+                    g_copy(2 + v, gb23[:, v], 0, P)
+            dz_interleave(scopy, g, S_MID, H)
 
         g = last
         h1_interleave(g)
-        if g - 1 not in TCS:
-            dzT_copy(g - 1, 1)
         dz_compute(g, 0)
-        dz_compute(g, 1)
         dzT_transpose(g, 0)
-        out0_half(g - 1, 0)
-        store(g - 1, 0, 2)
-        for m in range(3):
-            out1_pass(g - 2, m)
-        if SB:
-            for k in range(SW6, SW):
-                out1_pass(k, 3)
-        dz_compute(g, 2)
-        dz_compute(g, 3)
-        dzT_copy(g, 0)
+        out1_pass(g - 2, 2)
+        out1_pass(g - 2, 3)
+        dz_compute(g, 1)
         dzT_transpose(g, 1)
+        dzT_copy(vcopy, g, 0)
+        dzT_copy(scopy, g, 1)
         dzT_quant(g - 1, 1)
-        out0_half(g - 1, 1)
-        store(g - 1, 2, J)
-        dzT_quant(g, 0)
-        if not SB:
-            for k in range(SW6, SW):
-                out1_pass(k, 3)
-        dz_interleave(scopy, g, 0, TI)
-        dzT_copy(g, 1)
-        out0_half(g, 0)
-        store(g, 0, 1)
-        store(g, 1, 2)
-        for k in range(SW, g - 1):
-            out1_pass(k, 3)
+        out0_matmul(g - 1, 2)
+        out0_matmul(g - 1, 3)
         dz_quant(g - 1)
+        dzT_quant(g, 0)
+        dz_interleave(scopy, g, TAIL_V_COLS, H)
+        out0_copy(s_scale, g - 1, 2)
+        out0_copy(s_scale, g - 1, 3)
+        store(g - 1, 0, J)
+        out0_matmul(g, 0)
+        out0_matmul(g, 1)
+        for m in range(4):
+            out1_pass(g - 1, m)
+        dz_interleave(vcopy, g, 0, TAIL_V_COLS)
         dzT_quant(g, 1)
-        for m in range(QD):
-            out1_pass(g - 1, m)
         h1_quant(g)
-        dz_interleave(vcopy, g, TI, H)
         dz_quant(g)
-        out0_half(g, 1, emits=(out0_copy_s, out0_copy_v) if EV else None)
-        store(g, 2, 3)
-        store(g, 3, 4)
-        for m in range(QD, 4):
-            out1_pass(g - 1, m)
-        o1 = new([P, 4, H], F32, "o", OB)
-        o1_v = out_1.rearrange("(m p) w -> p m w", p=P)
+        out0_copy(s_scale, g, 0)
+        out0_copy(s_scale, g, 1)
+        store(g, 0, 2)
+        out0_matmul(g, 2)
+        out0_matmul(g, 3)
         for m in range(4):
             out1_pass(g, m)
+        out0_copy(s_scale, g, 2)
+        store(g, 2, 3)
+        out0_copy(v_scale, g, 3)
+        store(g, 3, 4)
+        o1 = new([P, 4 * H], F32, "stream", STREAM_BUFS)
         for m in range(4):
-            if m % 2 == 0:
-                nc.scalar.activation(out=o1[:, m, :], in_=acc[m][:], func=ACT.Copy, scale=0.125)
-            else:
-                nc.vector.tensor_scalar(out=o1[:, m, :], in0=acc[m][:], scalar1=0.125, scalar2=None, op0=ALU.mult)
-            nc.sync.dma_start(out=o1_v[:, m], in_=o1[:, m, :])
+            (s_scale if m % 2 == 0 else v_scale)(
+                o1[:, H * m:H * (m + 1)].rearrange("p (q u i) -> p u q i", u=2, i=16),
+                acc[m][:].rearrange("p (u q i) -> p u q i", u=2, i=16),
+            )
+            nc.sync.dma_start(out=o1_v[:, m], in_=o1[:, H * m:H * (m + 1)])

@@ -18,9 +18,10 @@ NODES = 512
 EDGES = 4096
 GROUPS = 8
 J = 4
-V_COLS = 64
-S_MID = 224
-TAIL_V_COLS = 384
+V_FIRST = 128
+V_COLS = 96
+S_MID = 240
+TAIL_V = 352
 STREAM_BUFS = 11
 BANKS = {"acc": 4, "ring": 3, "dh": 1}
 FMAX = (2.0 - 2.0 ** -23) * 2.0 ** 127
@@ -69,26 +70,33 @@ def tile_mpnnlayer_pb_v_kernel(tc, h1, h_V, mask_attend, W2, b2, W3, b3, z, grad
 
         z_t, h1_t = {}, {}
 
-        def load_group(g):
-            z_t[g] = new([P, J * H], F32, "stream", STREAM_BUFS)
-            nc.sync.dma_start(out=z_t[g][:, 0:2 * H], in_=z_v[:, g, 0:2 * H])
+        def load_z(g, half):
+            if half == 0:
+                z_t[g] = new([P, J * H], F32, "stream", STREAM_BUFS)
+            cols = slice(2 * H * half, 2 * H * (half + 1))
+            nc.sync.dma_start(out=z_t[g][:, cols], in_=z_v[:, g, cols])
+
+        def load_h1(g):
             h1_t[g] = load(h1_v[:, g], J * H, BF16, "h1", GROUPS)
-            nc.sync.dma_start(out=z_t[g][:, 2 * H:J * H], in_=z_v[:, g, 2 * H:J * H])
 
         w3_raw, w2_raw, g_raw = {}, {}, {}
         w3_raw[0] = load(w3_v[:, 0], 2 * H, BF16, "w_raw", 4)
         g_raw[0] = load(grad_v[:, 0], H, BF16, "g_raw", 4)
         w3_raw[1] = load(w3_v[:, 1], 2 * H, BF16, "w_raw", 4)
         nc.sync.dma_start(out=mk[0:GROUPS, :], in_=mask_v)
-        load_group(0)
         for b in range(2):
             w2_raw[b] = load(w2_v[:, b], 2 * H, BF16, "w_raw", 4)
-        g_raw[1] = load(grad_v[:, 1], H, BF16, "g_raw", 4)
-        load_group(1)
-        for t in (2, 3):
+        load_z(0, 0)
+        load_h1(1)
+        load_z(0, 1)
+        load_h1(0)
+        for t in (1, 2, 3):
             g_raw[t] = load(grad_v[:, t], H, BF16, "g_raw", 4)
-        for g in range(2, GROUPS):
-            load_group(g)
+        for g in range(1, GROUPS):
+            load_z(g, 0)
+            if g + 1 < GROUPS:
+                load_h1(g + 1)
+            load_z(g, 1)
 
         def transpose_stepped(dst, words):
             for u in range(2):
@@ -104,7 +112,7 @@ def tile_mpnnlayer_pb_v_kernel(tc, h1, h_V, mask_attend, W2, b2, W3, b3, z, grad
 
         def g_copy(t, bv, lo, hi):
             if t not in g_wide:
-                g_wide[t] = new([P, 2 * P * 4], BF16, "g_wide", 3)
+                g_wide[t] = new([P, 2 * P * 4], BF16, *(("h1i", 1) if t == 0 else ("g_wide", 3)))
             scopy(
                 out=g_wide[t][:].bitcast(F32).rearrange("p (r d u) -> p r d u", d=2, u=2)[:, lo:hi],
                 in_=bv[:, :, lo:hi].rearrange("p u r -> p r u").unsqueeze(2).to_broadcast([P, hi - lo, 2, 2]),
@@ -181,9 +189,12 @@ def tile_mpnnlayer_pb_v_kernel(tc, h1, h_V, mask_attend, W2, b2, W3, b3, z, grad
                 out=h1i_t[g][:].rearrange("p (w j) -> p w j", j=J), in0=h1_t[g][:].rearrange("p (j w) -> p w j", j=J),
                 scalar1=1.0, scalar2=0.0, op0=ALU.mult, op1=ALU.add)
 
+        def gcopy(out, in_):
+            nc.gpsimd.tensor_scalar(out=out, in0=in_, scalar1=1.0, scalar2=0.0, op0=ALU.mult, op1=ALU.add)
+
         def h1_quant(g):
-            h1c_t[g] = new([P, H], U32, "h1c", 3)
-            h1s_t[g] = new([P, H], U8, "h1s", 3)
+            h1c_t[g] = new([P, H], U32, "h1c", 4)
+            h1s_t[g] = new([P, H], U8, "h1s", 4)
             nc.vector.quantize_mx(out=h1c_t[g][:].bitcast(E4M3), scales=h1s_t[g][:], in_=h1i_t[g][:])
 
         def dz_compute(g, h):
@@ -201,10 +212,13 @@ def tile_mpnnlayer_pb_v_kernel(tc, h1, h_V, mask_attend, W2, b2, W3, b3, z, grad
 
         def dz_interleave(copy, g, lo, hi):
             if g not in dzi_t:
-                dzi_t[g] = new([P, J * H], BF16, "dzi", 2)
+                dzi_t[g] = new([P, J * H], BF16, *(("h1i", 1) if g == GROUPS - 2 else ("dzi", 2)))
             out = dzi_t[g][:].rearrange("p (w j) -> p w j", j=J)[:, lo:hi, :]
             in_ = dz_t[g][:].rearrange("p (j w) -> p w j", j=J)[:, lo:hi, :]
-            copy(out=out.rearrange("p (c i) j -> p c j i", i=4), in_=in_.rearrange("p (c i) j -> p c j i", i=4))
+            if g == GROUPS - 2 and lo == 0:
+                copy(out=out, in_=in_)
+            else:
+                copy(out=out.rearrange("p (c i) j -> p c j i", i=4), in_=in_.rearrange("p (c i) j -> p c j i", i=4))
 
         def dz_quant(g):
             dzc_t[g] = new([P, H], U32, "dzc", 3)
@@ -229,10 +243,10 @@ def tile_mpnnlayer_pb_v_kernel(tc, h1, h_V, mask_attend, W2, b2, W3, b3, z, grad
             ts_t[g, h] = new([P, 2 * P], U8, "tscl", 3)
             nc.vector.quantize_mx(out=tc_t[g, h][:].bitcast(E5M2), scales=ts_t[g, h][:], in_=dzT_t[g, h][:])
 
-        def out0_matmul(g, j):
+        def out0_matmul(g, j, tag="ring"):
             if j == 0:
                 o_t[g] = new([P, J * H], F32, "stream", STREAM_BUFS)
-            mm_t[g, j] = bank("ring")
+            mm_t[g, j] = bank(tag)
             h, v = divmod(j, 2)
             cols = slice(P * v, P * (v + 1))
             nc.tensor.matmul_mx(
@@ -269,110 +283,116 @@ def tile_mpnnlayer_pb_v_kernel(tc, h1, h_V, mask_attend, W2, b2, W3, b3, z, grad
 
         last = GROUPS - 1
 
-        h1_interleave(0)
+        w2_sorted = [w2_sort(b) for b in range(2)]
+        h1_interleave(1)
+        w2_banks = [w_bank(transpose_sorted, w2_sorted[b], "acc") for b in range(2)]
         dz_compute(0, 0)
         dzT_transpose(0, 0)
-        w2_sorted = [w2_sort(b) for b in range(2)]
-        w2a_bank = w_bank(transpose_sorted, w2_sorted[0], "acc")
+        w2_t = [w_copy(scopy, w2_banks[b]) for b in range(2)]
         dz_compute(0, 1)
         dzT_transpose(0, 1)
-        w2b_bank = w_bank(transpose_sorted, w2_sorted[1], "acc")
         dh_matmul(1)
-        gb1 = blocks(bank("acc"))[:, 0]
-        transpose_stepped(gb1, g_raw[1][:].bitcast(F32))
+        gb12 = blocks(bank("acc"))
+        gb3 = blocks(bank("acc"))
+        for t, dst in ((1, gb12[:, 0]), (2, gb12[:, 1]), (3, gb3[:, 0])):
+            transpose_stepped(dst, g_raw[t][:].bitcast(F32))
+        h1i_t[0] = new([P, J * H], BF16, "h1i_first")
+        scopy(
+            out=h1i_t[0][:].rearrange("p (c i j) -> p c j i", i=4, j=J),
+            in_=h1_t[0][:].rearrange("p (j c i) -> p c j i", i=4, j=J),
+        )
         dzT_copy(vcopy, 0, 0)
-        w2a = w_copy(scopy, w2a_bank)
-        w2b = w_copy(scopy, w2b_bank)
-        dz_interleave(vcopy, 0, 0, S_MID)
+        for b in range(2):
+            w_quant(w2_codes, w2_scl, b, w2_t[b])
         dzT_quant(0, 0)
-        w_quant(w2_codes, w2_scl, 0, w2a)
         dzT_copy(scopy, 0, 1)
-        w_quant(w2_codes, w2_scl, 1, w2b)
-        h1_quant(0)
-        g_copy(1, gb1, 0, P)
         out0_matmul(0, 0)
         out0_matmul(0, 1)
+        dz_interleave(vcopy, 0, 0, V_FIRST)
+        h1_quant(1)
+        dz_interleave(vcopy, 0, V_FIRST, V_FIRST + V_COLS)
+        g_copy(1, gb12[:, 0], 0, P)
+        g_copy(2, gb12[:, 1], 0, P)
+        g_copy(3, gb3[:, 0], 0, P)
         out0_copy(s_scale, 0, 0)
+        dz_interleave(scopy, 0, V_FIRST + V_COLS, H)
         out0_copy(s_scale, 0, 1)
-        dz_interleave(scopy, 0, S_MID, H)
+        store(0, 0, 2)
 
         for g in range(1, last):
-            h1_interleave(g)
+            h1_interleave(g + 1)
             dz_compute(g, 0)
             dzT_transpose(g, 0)
             out1_pass(g - 2, 2)
             out1_pass(g - 2, 3)
             dz_compute(g, 1)
             dzT_transpose(g, 1)
-            if g == 1:
-                gb23 = blocks(bank("acc"))
-                for v in range(2):
-                    transpose_stepped(gb23[:, v], g_raw[2 + v][:].bitcast(F32))
             dzT_copy(vcopy, g, 0)
+            dzT_copy(scopy, g, 1)
             if g <= 3:
                 g_quant(g, 0, P)
             dh_matmul(g + 1)
-            dzT_copy(scopy, g, 1)
             dzT_quant(g - 1, 1)
             out0_matmul(g - 1, 2)
             out0_matmul(g - 1, 3)
-            dz_interleave(vcopy, g, 0, V_COLS)
-            dz_interleave(scopy, g, V_COLS, S_MID)
             dzT_quant(g, 0)
-            out0_copy(s_scale, g - 1, 2)
-            out0_copy(s_scale, g - 1, 3)
-            store(g - 1, 0, J)
             out0_matmul(g, 0)
+            if g == 1:
+                h1_quant(0)
             dz_quant(g - 1)
             out1_pass(g - 1, 0)
+            h1_quant(g + 1)
+            if g < last - 1:
+                dz_interleave(vcopy, g, 0, V_COLS)
+                dz_interleave(scopy, g, V_COLS, S_MID)
+            else:
+                dzT_quant(g, 1)
+            out0_copy(s_scale, g - 1, 2)
             out0_matmul(g, 1)
             out1_pass(g - 1, 1)
-            h1_quant(g)
+            out0_copy(s_scale, g - 1, 3)
+            store(g - 1, 2, J)
             out0_copy(s_scale, g, 0)
-            out0_copy(s_scale, g, 1)
-            if g == 1:
-                for v in range(2):
-                    g_copy(2 + v, gb23[:, v], 0, P)
-            dz_interleave(scopy, g, S_MID, H)
+            if g < last - 1:
+                dz_interleave(scopy, g, S_MID, H)
+                out0_copy(s_scale, g, 1)
+                store(g, 0, 2)
 
         g = last
-        h1_interleave(g)
+        out0_matmul(g - 1, 2)
+        out1_pass(g - 2, 2)
+        out0_matmul(g - 1, 3)
+        out0_copy(s_scale, g - 1, 1)
+        store(g - 1, 0, 2)
+        dz_interleave(gcopy, g - 1, 0, H)
         dz_compute(g, 0)
         dzT_transpose(g, 0)
-        out1_pass(g - 2, 2)
-        out1_pass(g - 2, 3)
-        dz_compute(g, 1)
-        dzT_transpose(g, 1)
-        dzT_copy(vcopy, g, 0)
-        dzT_copy(scopy, g, 1)
-        dzT_quant(g - 1, 1)
-        out0_matmul(g - 1, 2)
-        out0_matmul(g - 1, 3)
-        dz_quant(g - 1)
-        dzT_quant(g, 0)
-        dz_interleave(scopy, g, TAIL_V_COLS, H)
         out0_copy(s_scale, g - 1, 2)
         out0_copy(s_scale, g - 1, 3)
-        store(g - 1, 0, J)
+        store(g - 1, 2, J)
+        dz_compute(g, 1)
+        dzT_transpose(g, 1)
+        out1_pass(g - 2, 3)
+        dzT_copy(vcopy, g, 0)
+        dzT_copy(scopy, g, 1)
+        dz_quant(g - 1)
+        dzT_quant(g, 0)
+        out1_pass(g - 1, 0)
         out0_matmul(g, 0)
         out0_matmul(g, 1)
-        for m in range(4):
+        for m in range(1, 4):
             out1_pass(g - 1, m)
-        dz_interleave(vcopy, g, 0, TAIL_V_COLS)
+        dz_interleave(scopy, g, TAIL_V, H)
+        dz_interleave(vcopy, g, 0, TAIL_V)
         dzT_quant(g, 1)
-        h1_quant(g)
         dz_quant(g)
-        out0_copy(s_scale, g, 0)
-        out0_copy(s_scale, g, 1)
-        store(g, 0, 2)
         out0_matmul(g, 2)
-        out0_matmul(g, 3)
+        out0_matmul(g, 3, "dh")
         for m in range(4):
             out1_pass(g, m)
-        out0_copy(s_scale, g, 2)
-        store(g, 2, 3)
-        out0_copy(v_scale, g, 3)
-        store(g, 3, 4)
+        for j in range(J):
+            out0_copy(s_scale if j < 3 else v_scale, g, j)
+            store(g, j, j + 1)
         o1 = new([P, 4 * H], F32, "stream", STREAM_BUFS)
         for m in range(4):
             (s_scale if m % 2 == 0 else v_scale)(

@@ -21,8 +21,10 @@ J = 4
 V_FIRST = 128
 V_COLS = 96
 S_MID = 240
+TAIL_A = 96
 TAIL_V = 352
 STREAM_BUFS = 11
+SPLIT_Z = 2
 BANKS = {"acc": 4, "ring": 3, "dh": 1}
 FMAX = (2.0 - 2.0 ** -23) * 2.0 ** 127
 
@@ -36,8 +38,8 @@ def tile_mpnnlayer_pb_v_kernel(tc, h1, h_V, mask_attend, W2, b2, W3, b3, z, grad
     z_v = z.rearrange("b n k w -> (b n k) w").rearrange("(g p j) w -> p g (j w)", p=P, j=J)
     o_v = out_0.rearrange("b n k w -> (b n k) w").rearrange("(g p j) w -> p g (j w)", p=P, j=J)
     mask_v = mask_attend.rearrange("b n k -> (b n k)").rearrange("(g c) -> g c", g=GROUPS)
-    grad_v = grad_out.rearrange("b n w -> (b n) w").rearrange("(t p) w -> p t w", p=P)
-    w2_v = W2.rearrange("(b r v) w -> r b (v w)", b=2, v=2)
+    grad_v = grad_out.rearrange("b n w -> (b n) w")
+    w2_v = W2.rearrange("(r v) w -> r (v w)", v=4)
     w3_v = W3.rearrange("(b r v) w -> r b (v w)", b=2, v=2)
     o1_v = out_1.rearrange("(m p) w -> p m w", p=P)
 
@@ -70,33 +72,32 @@ def tile_mpnnlayer_pb_v_kernel(tc, h1, h_V, mask_attend, W2, b2, W3, b3, z, grad
 
         z_t, h1_t = {}, {}
 
-        def load_z(g, half):
-            if half == 0:
+        def load_z(g, lo, hi):
+            if lo == 0:
                 z_t[g] = new([P, J * H], F32, "stream", STREAM_BUFS)
-            cols = slice(2 * H * half, 2 * H * (half + 1))
-            nc.sync.dma_start(out=z_t[g][:, cols], in_=z_v[:, g, cols])
+            nc.sync.dma_start(out=z_t[g][:, H * lo:H * hi], in_=z_v[:, g, H * lo:H * hi])
 
         def load_h1(g):
             h1_t[g] = load(h1_v[:, g], J * H, BF16, "h1", GROUPS)
 
-        w3_raw, w2_raw, g_raw = {}, {}, {}
-        w3_raw[0] = load(w3_v[:, 0], 2 * H, BF16, "w_raw", 4)
-        g_raw[0] = load(grad_v[:, 0], H, BF16, "g_raw", 4)
-        w3_raw[1] = load(w3_v[:, 1], 2 * H, BF16, "w_raw", 4)
+        w3_raw, g_raw = {}, {}
+        w3_raw[0] = load(w3_v[:, 0], 2 * H, BF16, "w_raw", 2)
+        g_raw[0] = load(grad_v[0:P], H, BF16, "g_first", 1)
+        w3_raw[1] = load(w3_v[:, 1], 2 * H, BF16, "w_raw", 2)
         nc.sync.dma_start(out=mk[0:GROUPS, :], in_=mask_v)
-        for b in range(2):
-            w2_raw[b] = load(w2_v[:, b], 2 * H, BF16, "w_raw", 4)
-        load_z(0, 0)
-        load_h1(1)
-        load_z(0, 1)
-        load_h1(0)
-        for t in (1, 2, 3):
-            g_raw[t] = load(grad_v[:, t], H, BF16, "g_raw", 4)
-        for g in range(1, GROUPS):
-            load_z(g, 0)
-            if g + 1 < GROUPS:
+        w2_raw = load(w2_v, 4 * H, BF16, "w2_raw", 1)
+        for g in range(GROUPS):
+            if g < SPLIT_Z:
+                load_z(g, 0, 2)
                 load_h1(g + 1)
-            load_z(g, 1)
+                load_z(g, 2, J)
+            else:
+                load_z(g, 0, J)
+            if g == 0:
+                load_h1(0)
+                g_rest = load(grad_v[P:NODES].rearrange("(r t) w -> r (t w)", t=3), 3 * H, BF16, "g_rest", 1)
+            if SPLIT_Z <= g + 1 < GROUPS - 1:
+                load_h1(g + 2)
 
         def transpose_stepped(dst, words):
             for u in range(2):
@@ -108,19 +109,22 @@ def tile_mpnnlayer_pb_v_kernel(tc, h1, h_V, mask_attend, W2, b2, W3, b3, z, grad
 
         g_codes = new([P, 2 * NODES], U32, "g_codes")
         g_scl = new([P, 2 * NODES], U8, "g_scl")
-        g_wide = {}
+        g_wide = new([P, 8 * P], BF16, "h1i", 1)
+        g_wide_rest = new([P, 8 * 3 * P], BF16, "g_wide_rest")
 
-        def g_copy(t, bv, lo, hi):
-            if t not in g_wide:
-                g_wide[t] = new([P, 2 * P * 4], BF16, *(("h1i", 1) if t == 0 else ("g_wide", 3)))
-            scopy(
-                out=g_wide[t][:].bitcast(F32).rearrange("p (r d u) -> p r d u", d=2, u=2)[:, lo:hi],
-                in_=bv[:, :, lo:hi].rearrange("p u r -> p r u").unsqueeze(2).to_broadcast([P, hi - lo, 2, 2]),
-            )
+        def g_copy(out, bv):
+            scopy(out=out, in_=bv.rearrange("p u r -> p r u").unsqueeze(2).to_broadcast(list(out.shape)))
 
-        def g_quant(t, lo, hi):
-            cols = slice(256 * t + 2 * lo, 256 * t + 2 * hi)
-            nc.vector.quantize_mx(out=g_codes[:, cols].bitcast(E5M2), scales=g_scl[:, cols], in_=g_wide[t][:, 8 * lo:8 * hi])
+        def g_first_copy(bv, lo, hi):
+            g_copy(g_wide[:].bitcast(F32).rearrange("p (r d u) -> p r d u", d=2, u=2)[:, lo:hi], bv[:, :, lo:hi])
+
+        def g_rest_copy(t, bv):
+            g_copy(g_wide_rest[:].bitcast(F32).rearrange("p (r t d u) -> p r t d u", t=3, d=2, u=2)[:, :, t], bv)
+
+        def g_quant(src, first, lo, hi):
+            cols = slice(2 * lo, 2 * hi)
+            nc.vector.quantize_mx(
+                out=g_codes[:, cols].bitcast(E5M2), scales=g_scl[:, cols], in_=src[:, 8 * (lo - first):8 * (hi - first)])
 
         def w_bank(transposer, raw, tag):
             bv = blocks(bank(tag))
@@ -141,7 +145,7 @@ def tile_mpnnlayer_pb_v_kernel(tc, h1, h_V, mask_attend, W2, b2, W3, b3, z, grad
             dst = new([P, 2 * H], BF16, "w2_sorted", 2)
             scopy(
                 out=dst[:].rearrange("p (v u q i) -> p v u q i", v=2, u=2, i=16),
-                in_=w2_raw[b][:].rearrange("p (v q u i) -> p v u q i", v=2, u=2, i=16),
+                in_=w2_raw[:, 2 * H * b:2 * H * (b + 1)].rearrange("p (v q u i) -> p v u q i", v=2, u=2, i=16),
             )
             return dst
 
@@ -152,12 +156,12 @@ def tile_mpnnlayer_pb_v_kernel(tc, h1, h_V, mask_attend, W2, b2, W3, b3, z, grad
         w3a = w_copy(vcopy, w_bank(transpose_stepped, w3_raw[0], "ring"))
         gb0 = blocks(bank("acc"))[:, 0]
         transpose_stepped(gb0, g_raw[0][:].bitcast(F32))
-        g_copy(0, gb0, 0, 64)
+        g_first_copy(gb0, 0, 64)
         w3b = w_copy(scopy, w_bank(transpose_stepped, w3_raw[1], "ring"))
         mv = blocks(bank("acc"))[:, 0]
         transpose_stepped(mv, mk[:].bitcast(F32))
         w_quant(w3_codes, w3_scl, 0, w3a)
-        g_quant(0, 0, 64)
+        g_quant(g_wide, 0, 0, 64)
         m_t = new([P, GROUPS * J], BF16, "m_t")
         vcopy(out=m_t[:].bitcast(F32).rearrange("p (g u) -> p g u", u=2), in_=mv[:, :, 0:GROUPS].rearrange("p u g -> p g u"))
         w_quant(w3_codes, w3_scl, 1, w3b)
@@ -177,8 +181,8 @@ def tile_mpnnlayer_pb_v_kernel(tc, h1, h_V, mask_attend, W2, b2, W3, b3, z, grad
             )
 
         dh_matmul(0)
-        g_copy(0, gb0, 64, P)
-        g_quant(0, 64, P)
+        g_first_copy(gb0, 64, P)
+        g_quant(g_wide, 0, 64, P)
 
         dz_t, dzi_t, dzc_t, dzs_t, h1i_t, h1c_t, h1s_t = {}, {}, {}, {}, {}, {}, {}
         tr_t, dzT_t, tc_t, ts_t, o_t, mm_t, acc = {}, {}, {}, {}, {}, {}, {}
@@ -288,22 +292,27 @@ def tile_mpnnlayer_pb_v_kernel(tc, h1, h_V, mask_attend, W2, b2, W3, b3, z, grad
         w2_banks = [w_bank(transpose_sorted, w2_sorted[b], "acc") for b in range(2)]
         dz_compute(0, 0)
         dzT_transpose(0, 0)
-        w2_t = [w_copy(scopy, w2_banks[b]) for b in range(2)]
+        w2_t = new([P, 4 * H], BF16, "w2_t")
+        for b in range(2):
+            scopy(
+                out=w2_t[:].bitcast(F32).rearrange("p (r b v u) -> p r b v u", b=2, v=2, u=2)[:, :, b],
+                in_=w2_banks[b].rearrange("p v u r -> p r v u"),
+            )
         dz_compute(0, 1)
         dzT_transpose(0, 1)
         dh_matmul(1)
         gb12 = blocks(bank("acc"))
         gb3 = blocks(bank("acc"))
-        for t, dst in ((1, gb12[:, 0]), (2, gb12[:, 1]), (3, gb3[:, 0])):
-            transpose_stepped(dst, g_raw[t][:].bitcast(F32))
+        g_banks = (gb12[:, 0], gb12[:, 1], gb3[:, 0])
+        for t in range(3):
+            transpose_stepped(g_banks[t], g_rest[:].bitcast(F32)[:, 256 * t:256 * (t + 1)])
         h1i_t[0] = new([P, J * H], BF16, "h1i_first")
         scopy(
             out=h1i_t[0][:].rearrange("p (c i j) -> p c j i", i=4, j=J),
             in_=h1_t[0][:].rearrange("p (j c i) -> p c j i", i=4, j=J),
         )
         dzT_copy(vcopy, 0, 0)
-        for b in range(2):
-            w_quant(w2_codes, w2_scl, b, w2_t[b])
+        nc.vector.quantize_mx(out=w2_codes[:].bitcast(E4M3), scales=w2_scl[:], in_=w2_t[:])
         dzT_quant(0, 0)
         dzT_copy(scopy, 0, 1)
         out0_matmul(0, 0)
@@ -311,13 +320,11 @@ def tile_mpnnlayer_pb_v_kernel(tc, h1, h_V, mask_attend, W2, b2, W3, b3, z, grad
         dz_interleave(vcopy, 0, 0, V_FIRST)
         h1_quant(1)
         dz_interleave(vcopy, 0, V_FIRST, V_FIRST + V_COLS)
-        g_copy(1, gb12[:, 0], 0, P)
-        g_copy(2, gb12[:, 1], 0, P)
-        g_copy(3, gb3[:, 0], 0, P)
+        for t in range(3):
+            g_rest_copy(t, g_banks[t])
         out0_copy(s_scale, 0, 0)
         dz_interleave(scopy, 0, V_FIRST + V_COLS, H)
         out0_copy(s_scale, 0, 1)
-        store(0, 0, 2)
 
         for g in range(1, last):
             h1_interleave(g + 1)
@@ -330,7 +337,7 @@ def tile_mpnnlayer_pb_v_kernel(tc, h1, h_V, mask_attend, W2, b2, W3, b3, z, grad
             dzT_copy(vcopy, g, 0)
             dzT_copy(scopy, g, 1)
             if g <= 3:
-                g_quant(g, 0, P)
+                g_quant(g_wide_rest, P, P * g, P * (g + 1))
             dh_matmul(g + 1)
             dzT_quant(g - 1, 1)
             out0_matmul(g - 1, 2)
@@ -349,18 +356,17 @@ def tile_mpnnlayer_pb_v_kernel(tc, h1, h_V, mask_attend, W2, b2, W3, b3, z, grad
                 dzT_quant(g, 1)
             out0_copy(s_scale, g - 1, 2)
             out0_matmul(g, 1)
-            out1_pass(g - 1, 1)
+            if g < last - 1:
+                out1_pass(g - 1, 1)
             out0_copy(s_scale, g - 1, 3)
-            store(g - 1, 2, J)
+            store(g - 1, 0, J)
             out0_copy(s_scale, g, 0)
             if g < last - 1:
                 dz_interleave(scopy, g, S_MID, H)
                 out0_copy(s_scale, g, 1)
-                store(g, 0, 2)
 
         g = last
         out0_matmul(g - 1, 2)
-        out1_pass(g - 2, 2)
         out0_matmul(g - 1, 3)
         out0_copy(s_scale, g - 1, 1)
         store(g - 1, 0, 2)
@@ -372,22 +378,24 @@ def tile_mpnnlayer_pb_v_kernel(tc, h1, h_V, mask_attend, W2, b2, W3, b3, z, grad
         store(g - 1, 2, J)
         dz_compute(g, 1)
         dzT_transpose(g, 1)
-        out1_pass(g - 2, 3)
+        for m in range(1, 4):
+            out1_pass(g - 2, m)
         dzT_copy(vcopy, g, 0)
         dzT_copy(scopy, g, 1)
-        dz_quant(g - 1)
+        dz_interleave(vcopy, g, 0, TAIL_A)
         dzT_quant(g, 0)
-        out1_pass(g - 1, 0)
         out0_matmul(g, 0)
         out0_matmul(g, 1)
+        dz_quant(g - 1)
+        dzT_quant(g, 1)
+        out1_pass(g - 1, 0)
+        out0_matmul(g, 2)
+        out0_matmul(g, 3, "dh")
         for m in range(1, 4):
             out1_pass(g - 1, m)
         dz_interleave(scopy, g, TAIL_V, H)
-        dz_interleave(vcopy, g, 0, TAIL_V)
-        dzT_quant(g, 1)
+        dz_interleave(vcopy, g, TAIL_A, TAIL_V)
         dz_quant(g)
-        out0_matmul(g, 2)
-        out0_matmul(g, 3, "dh")
         for m in range(4):
             out1_pass(g, m)
         for j in range(J):

@@ -24,7 +24,6 @@ S_MID = 240
 TAIL_A = 96
 TAIL_V = 352
 STREAM_BUFS = 11
-SPLIT_Z = 2
 BANKS = {"acc": 4, "ring": 3, "dh": 1}
 FMAX = (2.0 - 2.0 ** -23) * 2.0 ** 127
 
@@ -82,22 +81,24 @@ def tile_mpnnlayer_pb_v_kernel(tc, h1, h_V, mask_attend, W2, b2, W3, b3, z, grad
 
         w3_raw, g_raw = {}, {}
         w3_raw[0] = load(w3_v[:, 0], 2 * H, BF16, "w_raw", 2)
-        g_raw[0] = load(grad_v[0:P], H, BF16, "g_first", 1)
+        g_raw[0] = load(grad_v[0:P], H, BF16, "g_first", 2)
         w3_raw[1] = load(w3_v[:, 1], 2 * H, BF16, "w_raw", 2)
         nc.sync.dma_start(out=mk[0:GROUPS, :], in_=mask_v)
         w2_raw = load(w2_v, 4 * H, BF16, "w2_raw", 1)
-        for g in range(GROUPS):
-            if g < SPLIT_Z:
-                load_z(g, 0, 2)
+        load_z(0, 0, 2)
+        load_h1(1)
+        load_z(0, 2, J)
+        load_h1(0)
+        g_raw[1] = load(grad_v[P:2 * P], H, BF16, "g_first", 2)
+        load_z(1, 0, 2)
+        load_h1(2)
+        load_z(1, 2, J)
+        g_late = new([P, 2 * H], BF16, "g_late")
+        nc.sync.dma_start(out=g_late[:].rearrange("p (t w) -> p t w", t=2), in_=grad_v[2 * P:NODES].rearrange("(t p) w -> p t w", p=P))
+        for g in range(2, GROUPS):
+            if g + 1 < GROUPS:
                 load_h1(g + 1)
-                load_z(g, 2, J)
-            else:
-                load_z(g, 0, J)
-            if g == 0:
-                load_h1(0)
-                g_rest = load(grad_v[P:NODES].rearrange("(r t) w -> r (t w)", t=3), 3 * H, BF16, "g_rest", 1)
-            if SPLIT_Z <= g + 1 < GROUPS - 1:
-                load_h1(g + 2)
+            load_z(g, 0, J)
 
         def transpose_stepped(dst, words):
             for u in range(2):
@@ -119,7 +120,7 @@ def tile_mpnnlayer_pb_v_kernel(tc, h1, h_V, mask_attend, W2, b2, W3, b3, z, grad
             g_copy(g_wide[:].bitcast(F32).rearrange("p (r d u) -> p r d u", d=2, u=2)[:, lo:hi], bv[:, :, lo:hi])
 
         def g_rest_copy(t, bv):
-            g_copy(g_wide_rest[:].bitcast(F32).rearrange("p (r t d u) -> p r t d u", t=3, d=2, u=2)[:, :, t], bv)
+            g_copy(g_wide_rest[:].bitcast(F32).rearrange("p (t r d u) -> p t r d u", t=3, d=2, u=2)[:, t], bv)
 
         def g_quant(src, first, lo, hi):
             cols = slice(2 * lo, 2 * hi)
@@ -229,8 +230,8 @@ def tile_mpnnlayer_pb_v_kernel(tc, h1, h_V, mask_attend, W2, b2, W3, b3, z, grad
             dzs_t[g] = new([P, H], U8, "dzs", 3)
             nc.vector.quantize_mx(out=dzc_t[g][:].bitcast(E5M2), scales=dzs_t[g][:], in_=dzi_t[g][:])
 
-        def dzT_transpose(g, h):
-            tr_t[g, h] = blocks(bank("ring"))
+        def dzT_transpose(g, h, tag="ring"):
+            tr_t[g, h] = blocks(bank(tag))
             for v in range(2):
                 j = 2 * h + v
                 transpose_sorted(tr_t[g, h][:, v], dz_t[g][:].bitcast(F32)[:, 256 * j:256 * (j + 1)])
@@ -301,11 +302,8 @@ def tile_mpnnlayer_pb_v_kernel(tc, h1, h_V, mask_attend, W2, b2, W3, b3, z, grad
         dz_compute(0, 1)
         dzT_transpose(0, 1)
         dh_matmul(1)
-        gb12 = blocks(bank("acc"))
-        gb3 = blocks(bank("acc"))
-        g_banks = (gb12[:, 0], gb12[:, 1], gb3[:, 0])
-        for t in range(3):
-            transpose_stepped(g_banks[t], g_rest[:].bitcast(F32)[:, 256 * t:256 * (t + 1)])
+        gb1 = blocks(bank("acc"))[:, 0]
+        transpose_stepped(gb1, g_raw[1][:].bitcast(F32))
         h1i_t[0] = new([P, J * H], BF16, "h1i_first")
         scopy(
             out=h1i_t[0][:].rearrange("p (c i j) -> p c j i", i=4, j=J),
@@ -316,26 +314,34 @@ def tile_mpnnlayer_pb_v_kernel(tc, h1, h_V, mask_attend, W2, b2, W3, b3, z, grad
         dzT_quant(0, 0)
         dzT_copy(scopy, 0, 1)
         out0_matmul(0, 0)
-        out0_matmul(0, 1)
         dz_interleave(vcopy, 0, 0, V_FIRST)
         h1_quant(1)
         dz_interleave(vcopy, 0, V_FIRST, V_FIRST + V_COLS)
-        for t in range(3):
-            g_rest_copy(t, g_banks[t])
+        g_rest_copy(0, gb1)
         out0_copy(s_scale, 0, 0)
         dz_interleave(scopy, 0, V_FIRST + V_COLS, H)
-        out0_copy(s_scale, 0, 1)
 
         for g in range(1, last):
             h1_interleave(g + 1)
             dz_compute(g, 0)
             dzT_transpose(g, 0)
-            out1_pass(g - 2, 2)
-            out1_pass(g - 2, 3)
+            out0_matmul(g - 1, 1)
+            for m in range(2, 4):
+                out1_pass(g - 2, m)
+            out0_copy(s_scale, g - 1, 1)
+            if g == last - 1:
+                store(g - 1, 0, 2)
             dz_compute(g, 1)
             dzT_transpose(g, 1)
+            if g == 1:
+                gb23 = blocks(bank("acc"))
+                for v in range(2):
+                    transpose_stepped(gb23[:, v], g_late[:].bitcast(F32)[:, 256 * v:256 * (v + 1)])
             dzT_copy(vcopy, g, 0)
             dzT_copy(scopy, g, 1)
+            if g == 1:
+                for v in range(2):
+                    g_rest_copy(1 + v, gb23[:, v])
             if g <= 3:
                 g_quant(g_wide_rest, P, P * g, P * (g + 1))
             dh_matmul(g + 1)
@@ -347,7 +353,8 @@ def tile_mpnnlayer_pb_v_kernel(tc, h1, h_V, mask_attend, W2, b2, W3, b3, z, grad
             if g == 1:
                 h1_quant(0)
             dz_quant(g - 1)
-            out1_pass(g - 1, 0)
+            for m in range(2 if g < last - 1 else 1):
+                out1_pass(g - 1, m)
             h1_quant(g + 1)
             if g < last - 1:
                 dz_interleave(vcopy, g, 0, V_COLS)
@@ -355,29 +362,27 @@ def tile_mpnnlayer_pb_v_kernel(tc, h1, h_V, mask_attend, W2, b2, W3, b3, z, grad
             else:
                 dzT_quant(g, 1)
             out0_copy(s_scale, g - 1, 2)
-            out0_matmul(g, 1)
-            if g < last - 1:
-                out1_pass(g - 1, 1)
+            if g == last - 1:
+                out0_matmul(g, 1)
             out0_copy(s_scale, g - 1, 3)
-            store(g - 1, 0, J)
+            store(g - 1, 2 if g == last - 1 else 0, J)
             out0_copy(s_scale, g, 0)
             if g < last - 1:
                 dz_interleave(scopy, g, S_MID, H)
-                out0_copy(s_scale, g, 1)
 
         g = last
         out0_matmul(g - 1, 2)
-        out0_matmul(g - 1, 3)
-        out0_copy(s_scale, g - 1, 1)
-        store(g - 1, 0, 2)
         dz_interleave(gcopy, g - 1, 0, H)
         dz_compute(g, 0)
         dzT_transpose(g, 0)
+        out0_copy(s_scale, g - 1, 1)
+        store(g - 1, 0, 2)
+        out0_matmul(g - 1, 3)
         out0_copy(s_scale, g - 1, 2)
         out0_copy(s_scale, g - 1, 3)
         store(g - 1, 2, J)
         dz_compute(g, 1)
-        dzT_transpose(g, 1)
+        dzT_transpose(g, 1, "dh")
         for m in range(1, 4):
             out1_pass(g - 2, m)
         dzT_copy(vcopy, g, 0)
@@ -390,7 +395,7 @@ def tile_mpnnlayer_pb_v_kernel(tc, h1, h_V, mask_attend, W2, b2, W3, b3, z, grad
         dzT_quant(g, 1)
         out1_pass(g - 1, 0)
         out0_matmul(g, 2)
-        out0_matmul(g, 3, "dh")
+        out0_matmul(g, 3)
         for m in range(1, 4):
             out1_pass(g - 1, m)
         dz_interleave(scopy, g, TAIL_V, H)

@@ -329,8 +329,6 @@ def tile_mpnnlayer_pb_v_kernel(tc, h1, h_V, mask_attend, W2, b2, W3, b3, z, grad
             for m in range(2, 4):
                 out1_pass(g - 2, m)
             out0_copy(s_scale, g - 1, 1)
-            if g == last - 1:
-                store(g - 1, 0, 2)
             dz_compute(g, 1)
             dzT_transpose(g, 1)
             if g == 1:
@@ -365,7 +363,7 @@ def tile_mpnnlayer_pb_v_kernel(tc, h1, h_V, mask_attend, W2, b2, W3, b3, z, grad
             if g == last - 1:
                 out0_matmul(g, 1)
             out0_copy(s_scale, g - 1, 3)
-            store(g - 1, 2 if g == last - 1 else 0, J)
+            store(g - 1, 0, J)
             out0_copy(s_scale, g, 0)
             if g < last - 1:
                 dz_interleave(scopy, g, S_MID, H)
@@ -376,11 +374,10 @@ def tile_mpnnlayer_pb_v_kernel(tc, h1, h_V, mask_attend, W2, b2, W3, b3, z, grad
         dz_compute(g, 0)
         dzT_transpose(g, 0)
         out0_copy(s_scale, g - 1, 1)
-        store(g - 1, 0, 2)
         out0_matmul(g - 1, 3)
         out0_copy(s_scale, g - 1, 2)
         out0_copy(s_scale, g - 1, 3)
-        store(g - 1, 2, J)
+        store(g - 1, 0, J)
         dz_compute(g, 1)
         dzT_transpose(g, 1, "dh")
         for m in range(1, 4):
@@ -405,7 +402,8 @@ def tile_mpnnlayer_pb_v_kernel(tc, h1, h_V, mask_attend, W2, b2, W3, b3, z, grad
             out1_pass(g, m)
         for j in range(J):
             out0_copy(s_scale if j < 3 else v_scale, g, j)
-            store(g, j, j + 1)
+            if j % 2 == 1:
+                store(g, j - 1, j + 1)
         o1 = new([P, 4 * H], F32, "stream", STREAM_BUFS)
         for m in range(4):
             (s_scale if m % 2 == 0 else v_scale)(

@@ -19,12 +19,17 @@ EDGES = 4096
 GROUPS = 8
 J = 4
 V_FIRST = 128
-V_COLS = 96
-S_MID = 240
-TAIL_A = 96
-TAIL_V = 352
-STREAM_BUFS = 11
-BANKS = {"acc": 4, "ring": 3, "dh": 1}
+V_COLS = 0
+PE_COLS = 256
+S_MID = 320
+G_LAST = 128
+TAIL_V = 400
+V_SECOND = 128
+TAIL_B = 272
+TAIL_S = 400
+H1_SPLIT = 128
+H1_END = 256
+DH_BANK = 3
 FMAX = (2.0 - 2.0 ** -23) * 2.0 ** 127
 
 FLOPS = 2 * H * H * (NODES + EDGES + EDGES)
@@ -50,8 +55,13 @@ def tile_mpnnlayer_pb_v_kernel(tc, h1, h_V, mask_attend, W2, b2, W3, b3, z, grad
         def new(shape, dtype, tag, bufs=1):
             return sb.tile(shape, dtype, name=tag, tag=tag, bufs=bufs, align_bytes=64)
 
-        def bank(tag):
-            return ps.tile([P, 512], F32, name=tag, tag=tag, bufs=BANKS[tag])
+        ring = [4, 5, 6, 7]
+
+        def bank(k=None, dtype=F32, width=512):
+            if k is None:
+                k = ring.pop(0)
+                ring.append(k)
+            return ps.tile([P, width], dtype, name="bank%d" % k, tag="bank%d" % k, bufs=1)
 
         def blocks(bk):
             return bk[:].rearrange("p (v u r) -> p v u r", u=2, r=P)
@@ -61,6 +71,8 @@ def tile_mpnnlayer_pb_v_kernel(tc, h1, h_V, mask_attend, W2, b2, W3, b3, z, grad
 
         ident = new([P, P], F32, "ident")
         make_identity(nc, ident[:])
+        ident_bf = new([P, P], BF16, "ident_bf")
+        make_identity(nc, ident_bf[:])
         mk = new([P, H], BF16, "mk")
         nc.vector.memset(mk[:], 0.0)
 
@@ -73,7 +85,7 @@ def tile_mpnnlayer_pb_v_kernel(tc, h1, h_V, mask_attend, W2, b2, W3, b3, z, grad
 
         def load_z(g, lo, hi):
             if lo == 0:
-                z_t[g] = new([P, J * H], F32, "stream", STREAM_BUFS)
+                z_t[g] = new([P, J * H], F32, "rows%d" % g)
             nc.sync.dma_start(out=z_t[g][:, H * lo:H * hi], in_=z_v[:, g, H * lo:H * hi])
 
         def load_h1(g):
@@ -84,12 +96,12 @@ def tile_mpnnlayer_pb_v_kernel(tc, h1, h_V, mask_attend, W2, b2, W3, b3, z, grad
         g_raw[0] = load(grad_v[0:P], H, BF16, "g_first", 2)
         w3_raw[1] = load(w3_v[:, 1], 2 * H, BF16, "w_raw", 2)
         nc.sync.dma_start(out=mk[0:GROUPS, :], in_=mask_v)
+        g_raw[1] = load(grad_v[P:2 * P], H, BF16, "g_first", 2)
         w2_raw = load(w2_v, 4 * H, BF16, "w2_raw", 1)
         load_z(0, 0, 2)
         load_h1(1)
         load_z(0, 2, J)
         load_h1(0)
-        g_raw[1] = load(grad_v[P:2 * P], H, BF16, "g_first", 2)
         load_z(1, 0, 2)
         load_h1(2)
         load_z(1, 2, J)
@@ -154,13 +166,15 @@ def tile_mpnnlayer_pb_v_kernel(tc, h1, h_V, mask_attend, W2, b2, W3, b3, z, grad
         w3_scl = new([P, H], U8, "w3_scl")
         w2_codes = new([P, H], U32, "w2_codes")
         w2_scl = new([P, H], U8, "w2_scl")
-        w3a = w_copy(vcopy, w_bank(transpose_stepped, w3_raw[0], "ring"))
-        gb0 = blocks(bank("acc"))[:, 0]
+        w3a = w_copy(vcopy, w_bank(transpose_stepped, w3_raw[0], None))
+        gb0 = blocks(bank(0))[:, 0]
         transpose_stepped(gb0, g_raw[0][:].bitcast(F32))
         g_first_copy(gb0, 0, 64)
-        w3b = w_copy(scopy, w_bank(transpose_stepped, w3_raw[1], "ring"))
-        mv = blocks(bank("acc"))[:, 0]
+        w3b = w_copy(scopy, w_bank(transpose_stepped, w3_raw[1], None))
+        mv = blocks(bank(1))[:, 0]
         transpose_stepped(mv, mk[:].bitcast(F32))
+        gb1 = blocks(bank(2))[:, 0]
+        transpose_stepped(gb1, g_raw[1][:].bitcast(F32))
         w_quant(w3_codes, w3_scl, 0, w3a)
         g_quant(g_wide, 0, 0, 64)
         m_t = new([P, GROUPS * J], BF16, "m_t")
@@ -172,7 +186,7 @@ def tile_mpnnlayer_pb_v_kernel(tc, h1, h_V, mask_attend, W2, b2, W3, b3, z, grad
         dh_t = {}
 
         def dh_matmul(g):
-            dh_t[g] = bank("dh")
+            dh_t[g] = bank(DH_BANK)
             cols = slice(P * g, P * (g + 1))
             nc.tensor.matmul_mx(
                 out=dh_t[g][:],
@@ -184,6 +198,8 @@ def tile_mpnnlayer_pb_v_kernel(tc, h1, h_V, mask_attend, W2, b2, W3, b3, z, grad
         dh_matmul(0)
         g_first_copy(gb0, 64, P)
         g_quant(g_wide, 0, 64, P)
+        g_rest_copy(0, gb1)
+        g_quant(g_wide_rest, P, P, 2 * P)
 
         dz_t, dzi_t, dzc_t, dzs_t, h1i_t, h1c_t, h1s_t = {}, {}, {}, {}, {}, {}, {}
         tr_t, dzT_t, tc_t, ts_t, o_t, mm_t, acc = {}, {}, {}, {}, {}, {}, {}
@@ -198,39 +214,65 @@ def tile_mpnnlayer_pb_v_kernel(tc, h1, h_V, mask_attend, W2, b2, W3, b3, z, grad
             nc.gpsimd.tensor_scalar(out=out, in0=in_, scalar1=1.0, scalar2=0.0, op0=ALU.mult, op1=ALU.add)
 
         def h1_quant(g):
-            h1c_t[g] = new([P, H], U32, "h1c", 4)
-            h1s_t[g] = new([P, H], U8, "h1s", 4)
+            h1c_t[g] = new([P, H], U32, "h1c", GROUPS)
+            h1s_t[g] = new([P, H], U8, "h1s", GROUPS)
             nc.vector.quantize_mx(out=h1c_t[g][:].bitcast(E4M3), scales=h1s_t[g][:], in_=h1i_t[g][:])
 
-        def dz_compute(g, h):
-            if h == 0:
+        def dz_piece(g, j, u):
+            if g not in dz_t:
                 dz_t[g] = new([P, J * H], BF16, "dz", 3)
+            nc.vector.scalar_tensor_tensor(
+                out=dz_t[g][:, H * j + 256 * u:H * j + 256 * (u + 1)].rearrange("p (q i) -> p q i", i=16),
+                in0=z_t[g][:, H * j:H * (j + 1)].rearrange("p (q u i) -> p q u i", u=2, i=16)[:, :, u, :],
+                scalar=thr[:, J * g + j:J * g + j + 1],
+                in1=dh_t[g][:].rearrange("p (q u i) -> p q u i", u=2, i=16)[:, :, u, :],
+                op0=ALU.is_gt, op1=ALU.mult,
+            )
+
+        def dz_compute(g, h):
             for j in (2 * h, 2 * h + 1):
                 for u in range(2):
-                    nc.vector.scalar_tensor_tensor(
-                        out=dz_t[g][:, H * j + 256 * u:H * j + 256 * (u + 1)].rearrange("p (q i) -> p q i", i=16),
-                        in0=z_t[g][:, H * j:H * (j + 1)].rearrange("p (q u i) -> p q u i", u=2, i=16)[:, :, u, :],
-                        scalar=thr[:, J * g + j:J * g + j + 1],
-                        in1=dh_t[g][:].rearrange("p (q u i) -> p q u i", u=2, i=16)[:, :, u, :],
-                        op0=ALU.is_gt, op1=ALU.mult,
-                    )
+                    dz_piece(g, j, u)
 
         def dz_interleave(copy, g, lo, hi):
             if g not in dzi_t:
-                dzi_t[g] = new([P, J * H], BF16, *(("h1i", 1) if g == GROUPS - 2 else ("dzi", 2)))
+                dzi_t[g] = new([P, J * H], BF16, "dzi", 2)
+            if hi <= lo:
+                return
             out = dzi_t[g][:].rearrange("p (w j) -> p w j", j=J)[:, lo:hi, :]
             in_ = dz_t[g][:].rearrange("p (j w) -> p w j", j=J)[:, lo:hi, :]
-            if g == GROUPS - 2 and lo == 0:
+            if copy is gcopy:
                 copy(out=out, in_=in_)
             else:
                 copy(out=out.rearrange("p (c i) j -> p c j i", i=4), in_=in_.rearrange("p (c i) j -> p c j i", i=4))
 
-        def dz_quant(g):
-            dzc_t[g] = new([P, H], U32, "dzc", 3)
-            dzs_t[g] = new([P, H], U8, "dzs", 3)
-            nc.vector.quantize_mx(out=dzc_t[g][:].bitcast(E5M2), scales=dzs_t[g][:], in_=dzi_t[g][:])
+        pe_t = {}
 
-        def dzT_transpose(g, h, tag="ring"):
+        def pe_rows(src, lo, dst):
+            for c in range(0, PE_COLS, P):
+                nc.tensor.matmul(
+                    dst[:, J * c:J * (c + P)].rearrange("p (w j) -> p w j", j=J), lhsT=ident_bf[:],
+                    rhs=src[:].rearrange("p (j w) -> p w j", j=J)[:, lo + c:lo + c + P, :], start=True, stop=True)
+            return dst
+
+        def pe_interleave(g):
+            pe_t[g] = pe_rows(dz_t[g], 0, bank(None, BF16, J * PE_COLS))
+
+        def pe_copy(g):
+            if g not in dzi_t:
+                dzi_t[g] = new([P, J * H], BF16, "dzi", 2)
+            scopy(out=dzi_t[g][:, 0:J * PE_COLS], in_=pe_t[g][:])
+
+        def dz_quant_part(g, lo, hi, src):
+            if g not in dzc_t:
+                dzc_t[g] = new([P, H], U32, "dzc", GROUPS)
+                dzs_t[g] = new([P, H], U8, "dzs", GROUPS)
+            nc.vector.quantize_mx(out=dzc_t[g][:, lo:hi].bitcast(E5M2), scales=dzs_t[g][:, lo:hi], in_=src)
+
+        def dz_quant(g):
+            dz_quant_part(g, 0, H, dzi_t[g][:])
+
+        def dzT_transpose(g, h, tag=None):
             tr_t[g, h] = blocks(bank(tag))
             for v in range(2):
                 j = 2 * h + v
@@ -248,9 +290,9 @@ def tile_mpnnlayer_pb_v_kernel(tc, h1, h_V, mask_attend, W2, b2, W3, b3, z, grad
             ts_t[g, h] = new([P, 2 * P], U8, "tscl", 3)
             nc.vector.quantize_mx(out=tc_t[g, h][:].bitcast(E5M2), scales=ts_t[g, h][:], in_=dzT_t[g, h][:])
 
-        def out0_matmul(g, j, tag="ring"):
+        def out0_matmul(g, j, tag=None):
             if j == 0:
-                o_t[g] = new([P, J * H], F32, "stream", STREAM_BUFS)
+                o_t[g] = new([P, J * H], F32, "rows%d" % g)
             mm_t[g, j] = bank(tag)
             h, v = divmod(j, 2)
             cols = slice(P * v, P * (v + 1))
@@ -274,7 +316,7 @@ def tile_mpnnlayer_pb_v_kernel(tc, h1, h_V, mask_attend, W2, b2, W3, b3, z, grad
             if g < 0:
                 return
             if g == 0:
-                acc[m] = bank("acc")
+                acc[m] = bank(m if m < 3 else ring.pop(0))
             cols = slice(P * m, P * (m + 1))
             nc.tensor.matmul_mx(
                 out=acc[m][:],
@@ -290,7 +332,7 @@ def tile_mpnnlayer_pb_v_kernel(tc, h1, h_V, mask_attend, W2, b2, W3, b3, z, grad
 
         w2_sorted = [w2_sort(b) for b in range(2)]
         h1_interleave(1)
-        w2_banks = [w_bank(transpose_sorted, w2_sorted[b], "acc") for b in range(2)]
+        w2_banks = [w_bank(transpose_sorted, w2_sorted[b], (1, 0)[b]) for b in range(2)]
         dz_compute(0, 0)
         dzT_transpose(0, 0)
         w2_t = new([P, 4 * H], BF16, "w2_t")
@@ -302,109 +344,133 @@ def tile_mpnnlayer_pb_v_kernel(tc, h1, h_V, mask_attend, W2, b2, W3, b3, z, grad
         dz_compute(0, 1)
         dzT_transpose(0, 1)
         dh_matmul(1)
-        gb1 = blocks(bank("acc"))[:, 0]
-        transpose_stepped(gb1, g_raw[1][:].bitcast(F32))
         h1i_t[0] = new([P, J * H], BF16, "h1i_first")
-        scopy(
-            out=h1i_t[0][:].rearrange("p (c i j) -> p c j i", i=4, j=J),
-            in_=h1_t[0][:].rearrange("p (j c i) -> p c j i", i=4, j=J),
-        )
+
+        def h1_first(lo, hi):
+            if hi <= lo:
+                return
+            scopy(
+                out=h1i_t[0][:].rearrange("p (c i j) -> p c j i", i=4, j=J)[:, lo // 4:hi // 4],
+                in_=h1_t[0][:].rearrange("p (j c i) -> p c j i", i=4, j=J)[:, lo // 4:hi // 4],
+            )
+
         dzT_copy(vcopy, 0, 0)
-        nc.vector.quantize_mx(out=w2_codes[:].bitcast(E4M3), scales=w2_scl[:], in_=w2_t[:])
-        dzT_quant(0, 0)
+        h1_first(0, H1_SPLIT)
         dzT_copy(scopy, 0, 1)
+        nc.vector.quantize_mx(out=w2_codes[:].bitcast(E4M3), scales=w2_scl[:], in_=w2_t[:])
+        pe_interleave(0)
+        dzT_quant(0, 0)
         out0_matmul(0, 0)
-        dz_interleave(vcopy, 0, 0, V_FIRST)
+        out0_matmul(0, 1)
+        dz_interleave(vcopy, 0, H - V_FIRST, H)
+        h1_first(H1_SPLIT, H1_END)
         h1_quant(1)
-        dz_interleave(vcopy, 0, V_FIRST, V_FIRST + V_COLS)
-        g_rest_copy(0, gb1)
-        out0_copy(s_scale, 0, 0)
-        dz_interleave(scopy, 0, V_FIRST + V_COLS, H)
+        dzT_quant(0, 1)
 
         for g in range(1, last):
             h1_interleave(g + 1)
             dz_compute(g, 0)
+            out0_matmul(g - 1, 2)
+            out1_pass(g - 2, 0)
+            out1_pass(g - 2, 1)
+            if g == 1:
+                h1_bank = pe_rows(h1_t[0], H - PE_COLS, bank(0, BF16, J * PE_COLS))
+            pe_copy(g - 1)
             dzT_transpose(g, 0)
-            out0_matmul(g - 1, 1)
-            for m in range(2, 4):
-                out1_pass(g - 2, m)
+            out0_copy(s_scale, g - 1, 0)
+            out0_matmul(g - 1, 3)
+            out1_pass(g - 2, 2)
             out0_copy(s_scale, g - 1, 1)
+            if g == 1:
+                dz_interleave(scopy, 0, PE_COLS, H - V_FIRST)
             dz_compute(g, 1)
             dzT_transpose(g, 1)
             if g == 1:
-                gb23 = blocks(bank("acc"))
+                gb23 = blocks(bank(1))
                 for v in range(2):
                     transpose_stepped(gb23[:, v], g_late[:].bitcast(F32)[:, 256 * v:256 * (v + 1)])
-            dzT_copy(vcopy, g, 0)
-            dzT_copy(scopy, g, 1)
-            if g == 1:
-                for v in range(2):
-                    g_rest_copy(1 + v, gb23[:, v])
-            if g <= 3:
-                g_quant(g_wide_rest, P, P * g, P * (g + 1))
-            dh_matmul(g + 1)
-            dzT_quant(g - 1, 1)
-            out0_matmul(g - 1, 2)
-            out0_matmul(g - 1, 3)
-            dzT_quant(g, 0)
-            out0_matmul(g, 0)
-            if g == 1:
-                h1_quant(0)
-            dz_quant(g - 1)
-            for m in range(2 if g < last - 1 else 1):
-                out1_pass(g - 1, m)
-            h1_quant(g + 1)
-            if g < last - 1:
-                dz_interleave(vcopy, g, 0, V_COLS)
-                dz_interleave(scopy, g, V_COLS, S_MID)
-            else:
-                dzT_quant(g, 1)
             out0_copy(s_scale, g - 1, 2)
-            if g == last - 1:
-                out0_matmul(g, 1)
             out0_copy(s_scale, g - 1, 3)
             store(g - 1, 0, J)
-            out0_copy(s_scale, g, 0)
+            if g == 1:
+                scopy(out=h1i_t[0][:, J * (H - PE_COLS):], in_=h1_bank[:])
+            dzT_copy(vcopy, g, 0)
+            if g > 1:
+                dz_interleave(scopy, g, PE_COLS, S_MID)
+            dzT_copy(scopy, g, 1)
+            if g == 1:
+                h1_first(H1_END, H - PE_COLS)
+                g_rest_copy(1, gb23[:, 0])
+                g_rest_copy(2, gb23[:, 1])
+            if g in (2, 3):
+                g_quant(g_wide_rest, P, P * g, P * (g + 1))
+            dh_matmul(g + 1)
+            dz_quant(g - 1)
             if g < last - 1:
-                dz_interleave(scopy, g, S_MID, H)
+                pe_interleave(g)
+            else:
+                for k in range(4):
+                    out1_pass(k, 3)
+            dzT_quant(g, 0)
+            out0_matmul(g, 0)
+            out0_matmul(g, 1)
+            dz_interleave(vcopy, g, H - (V_SECOND if g == 1 else V_COLS), H)
+            dz_interleave(scopy, g, PE_COLS if g == 1 else S_MID, H - (V_SECOND if g == 1 else V_COLS))
+            if g == 1:
+                h1_quant(0)
+            h1_quant(g + 1)
+            dzT_quant(g, 1)
 
         g = last
-        out0_matmul(g - 1, 2)
-        dz_interleave(gcopy, g - 1, 0, H)
+        gp_t = new([P, J * PE_COLS], BF16, "h1i", 1)
+        gcopy(gp_t[:].rearrange("p (w j) -> p w j", j=J), dz_t[g - 1][:].rearrange("p (j w) -> p w j", j=J)[:, 0:PE_COLS])
         dz_compute(g, 0)
+        out0_matmul(g - 1, 2)
+        out1_pass(g - 2, 0)
+        out1_pass(g - 2, 1)
+        out0_copy(s_scale, g - 1, 0)
         dzT_transpose(g, 0)
         out0_copy(s_scale, g - 1, 1)
         out0_matmul(g - 1, 3)
+        out1_pass(g - 2, 2)
+        out1_pass(4, 3)
         out0_copy(s_scale, g - 1, 2)
         out0_copy(s_scale, g - 1, 3)
         store(g - 1, 0, J)
-        dz_compute(g, 1)
-        dzT_transpose(g, 1, "dh")
-        for m in range(1, 4):
-            out1_pass(g - 2, m)
+        dz_piece(g, 2, 0)
+        dz_piece(g, 3, 0)
+        dz_interleave(gcopy, g, 0, G_LAST)
+        dz_piece(g, 2, 1)
+        dz_piece(g, 3, 1)
+        dzT_transpose(g, 1, DH_BANK)
+        out1_pass(5, 3)
         dzT_copy(vcopy, g, 0)
+        dz_interleave(scopy, g, TAIL_S, H)
         dzT_copy(scopy, g, 1)
-        dz_interleave(vcopy, g, 0, TAIL_A)
+        dz_quant_part(g - 1, PE_COLS, H, dzi_t[g - 1][:, J * PE_COLS:])
         dzT_quant(g, 0)
         out0_matmul(g, 0)
         out0_matmul(g, 1)
-        dz_quant(g - 1)
-        dzT_quant(g, 1)
+        dz_quant_part(g - 1, 0, PE_COLS, gp_t[:])
         out1_pass(g - 1, 0)
+        out1_pass(g - 1, 1)
+        dz_interleave(scopy, g, TAIL_V, TAIL_S)
+        dz_interleave(vcopy, g, G_LAST, TAIL_B)
+        dzT_quant(g, 1)
+        out1_pass(g - 1, 2)
         out0_matmul(g, 2)
-        out0_matmul(g, 3)
-        for m in range(1, 4):
-            out1_pass(g - 1, m)
-        dz_interleave(scopy, g, TAIL_V, H)
-        dz_interleave(vcopy, g, TAIL_A, TAIL_V)
+        out0_copy(s_scale, g, 0)
+        store(g, 0, 1)
+        out0_matmul(g, 3, DH_BANK)
+        out1_pass(g - 1, 3)
+        dz_interleave(vcopy, g, TAIL_B, TAIL_V)
         dz_quant(g)
         for m in range(4):
             out1_pass(g, m)
-        for j in range(J):
+        for j in range(1, J):
             out0_copy(s_scale if j < 3 else v_scale, g, j)
-            if j % 2 == 1:
-                store(g, j - 1, j + 1)
-        o1 = new([P, 4 * H], F32, "stream", STREAM_BUFS)
+            store(g, j, j + 1)
+        o1 = new([P, 4 * H], F32, "rows0")
         for m in range(4):
             (s_scale if m % 2 == 0 else v_scale)(
                 o1[:, H * m:H * (m + 1)].rearrange("p (q u i) -> p u q i", u=2, i=16),

@@ -251,8 +251,9 @@ def tile_mpnnlayer_pb_v_kernel(tc, h1, h_V, mask_attend, W2, b2, W3, b3, z, grad
         def pe_rows(src, lo, dst):
             for c in range(0, PE_COLS, P):
                 nc.tensor.matmul(
-                    dst[:, J * c:J * (c + P)].rearrange("p (w j) -> p w j", j=J), lhsT=ident_bf[:],
-                    rhs=src[:].rearrange("p (j w) -> p w j", j=J)[:, lo + c:lo + c + P, :], start=True, stop=True)
+                    dst[:, J * c:J * (c + P)].rearrange("p (c i j) -> p c j i", i=8, j=J), lhsT=ident_bf[:],
+                    rhs=src[:].rearrange("p (j w) -> p j w", j=J)[:, :, lo + c:lo + c + P].rearrange("p j (c i) -> p c j i", i=8),
+                    start=True, stop=True)
             return dst
 
         def pe_interleave(g):

@@ -18,17 +18,18 @@ NODES = 512
 EDGES = 4096
 GROUPS = 8
 J = 4
-V_FIRST = 128
+V_FIRST = 64
 V_COLS = 0
 PE_COLS = 256
-S_MID = 320
+S_MID = 256
 G_LAST = 128
-TAIL_V = 400
-V_SECOND = 128
-TAIL_B = 272
-TAIL_S = 400
+TAIL_V = 304
+V_SECOND = 192
+TAIL_S = 352
 H1_SPLIT = 128
 H1_END = 256
+S_FIRST = 384
+G_PREV = 384
 DH_BANK = 3
 FMAX = (2.0 - 2.0 ** -23) * 2.0 ** 127
 
@@ -248,16 +249,16 @@ def tile_mpnnlayer_pb_v_kernel(tc, h1, h_V, mask_attend, W2, b2, W3, b3, z, grad
 
         pe_t = {}
 
-        def pe_rows(src, lo, dst):
-            for c in range(0, PE_COLS, P):
-                nc.tensor.matmul(
-                    dst[:, J * c:J * (c + P)].rearrange("p (c i j) -> p c j i", i=8, j=J), lhsT=ident_bf[:],
-                    rhs=src[:].rearrange("p (j w) -> p j w", j=J)[:, :, lo + c:lo + c + P].rearrange("p j (c i) -> p c j i", i=8),
-                    start=True, stop=True)
-            return dst
+        def pe_rows(src, lo, dst, c):
+            nc.tensor.matmul(
+                dst[:, J * c:J * (c + P)].rearrange("p (c i j) -> p c j i", i=8, j=J), lhsT=ident_bf[:],
+                rhs=src[:].rearrange("p (j w) -> p j w", j=J)[:, :, lo + c:lo + c + P].rearrange("p j (c i) -> p c j i", i=8),
+                start=True, stop=True)
 
         def pe_interleave(g):
-            pe_t[g] = pe_rows(dz_t[g], 0, bank(None, BF16, J * PE_COLS))
+            pe_t[g] = bank(None, BF16, J * PE_COLS)
+            for c in range(0, PE_COLS, P):
+                pe_rows(dz_t[g], 0, pe_t[g], c)
 
         def pe_copy(g):
             if g not in dzi_t:
@@ -365,6 +366,7 @@ def tile_mpnnlayer_pb_v_kernel(tc, h1, h_V, mask_attend, W2, b2, W3, b3, z, grad
         out0_matmul(0, 1)
         dz_interleave(vcopy, 0, H - V_FIRST, H)
         h1_first(H1_SPLIT, H1_END)
+        dz_interleave(scopy, 0, PE_COLS, S_FIRST)
         h1_quant(1)
         dzT_quant(0, 1)
 
@@ -375,15 +377,18 @@ def tile_mpnnlayer_pb_v_kernel(tc, h1, h_V, mask_attend, W2, b2, W3, b3, z, grad
             out1_pass(g - 2, 0)
             out1_pass(g - 2, 1)
             if g == 1:
-                h1_bank = pe_rows(h1_t[0], H - PE_COLS, bank(0, BF16, J * PE_COLS))
+                h1_bank = bank(0, BF16, J * PE_COLS)
+                pe_rows(h1_t[0], H - PE_COLS, h1_bank, 0)
             pe_copy(g - 1)
             dzT_transpose(g, 0)
+            if g == 1:
+                pe_rows(h1_t[0], H - PE_COLS, h1_bank, P)
             out0_copy(s_scale, g - 1, 0)
             out0_matmul(g - 1, 3)
             out1_pass(g - 2, 2)
             out0_copy(s_scale, g - 1, 1)
             if g == 1:
-                dz_interleave(scopy, 0, PE_COLS, H - V_FIRST)
+                dz_interleave(scopy, 0, S_FIRST, H - V_FIRST)
             dz_compute(g, 1)
             dzT_transpose(g, 1)
             if g == 1:
@@ -391,12 +396,12 @@ def tile_mpnnlayer_pb_v_kernel(tc, h1, h_V, mask_attend, W2, b2, W3, b3, z, grad
                 for v in range(2):
                     transpose_stepped(gb23[:, v], g_late[:].bitcast(F32)[:, 256 * v:256 * (v + 1)])
             out0_copy(s_scale, g - 1, 2)
-            out0_copy(s_scale, g - 1, 3)
-            store(g - 1, 0, J)
             if g == 1:
                 scopy(out=h1i_t[0][:, J * (H - PE_COLS):], in_=h1_bank[:])
+            out0_copy(s_scale, g - 1, 3)
+            store(g - 1, 0, J)
             dzT_copy(vcopy, g, 0)
-            if g > 1:
+            if 1 < g < last - 1:
                 dz_interleave(scopy, g, PE_COLS, S_MID)
             dzT_copy(scopy, g, 1)
             if g == 1:
@@ -410,61 +415,73 @@ def tile_mpnnlayer_pb_v_kernel(tc, h1, h_V, mask_attend, W2, b2, W3, b3, z, grad
             if g < last - 1:
                 pe_interleave(g)
             else:
-                for k in range(4):
+                for k in range(3):
                     out1_pass(k, 3)
             dzT_quant(g, 0)
             out0_matmul(g, 0)
             out0_matmul(g, 1)
+            if g == last - 1:
+                out1_pass(3, 3)
             dz_interleave(vcopy, g, H - (V_SECOND if g == 1 else V_COLS), H)
-            dz_interleave(scopy, g, PE_COLS if g == 1 else S_MID, H - (V_SECOND if g == 1 else V_COLS))
+            dz_interleave(scopy, g, {1: PE_COLS, last - 1: G_PREV}.get(g, S_MID), H - (V_SECOND if g == 1 else V_COLS))
             if g == 1:
                 h1_quant(0)
             h1_quant(g + 1)
             dzT_quant(g, 1)
 
         g = last
-        gp_t = new([P, J * PE_COLS], BF16, "h1i", 1)
-        gcopy(gp_t[:].rearrange("p (w j) -> p w j", j=J), dz_t[g - 1][:].rearrange("p (j w) -> p w j", j=J)[:, 0:PE_COLS])
+        gp_t = new([P, J * G_PREV], BF16, "h1i", 1)
+        gcopy(gp_t[:].rearrange("p (w j) -> p w j", j=J), dz_t[g - 1][:].rearrange("p (j w) -> p w j", j=J)[:, 0:G_PREV])
         dz_compute(g, 0)
         out0_matmul(g - 1, 2)
         out1_pass(g - 2, 0)
-        out1_pass(g - 2, 1)
         out0_copy(s_scale, g - 1, 0)
-        dzT_transpose(g, 0)
         out0_copy(s_scale, g - 1, 1)
+        store(g - 1, 0, 2)
         out0_matmul(g - 1, 3)
+        dzT_transpose(g, 0)
+        out1_pass(g - 2, 1)
         out1_pass(g - 2, 2)
-        out1_pass(4, 3)
         out0_copy(s_scale, g - 1, 2)
         out0_copy(s_scale, g - 1, 3)
-        store(g - 1, 0, J)
+        store(g - 1, 2, J)
         dz_piece(g, 2, 0)
         dz_piece(g, 3, 0)
         dz_interleave(gcopy, g, 0, G_LAST)
         dz_piece(g, 2, 1)
         dz_piece(g, 3, 1)
         dzT_transpose(g, 1, DH_BANK)
-        out1_pass(5, 3)
-        dzT_copy(vcopy, g, 0)
+        out1_pass(4, 3)
+        dzT_t[g, 0] = new([P, 2 * P * 4], BF16, "dzT", 3)
+        tc_t[g, 0] = new([P, 2 * P], U32, "tcod", 3)
+        ts_t[g, 0] = new([P, 2 * P], U8, "tscl", 3)
+        for v in range(2):
+            vcopy(
+                out=dzT_t[g, 0][:, H * v:H * (v + 1)].bitcast(F32).rearrange("p (r u) -> p r u", u=2),
+                in_=tr_t[g, 0][:, v].rearrange("p u r -> p r u"),
+            )
         dz_interleave(scopy, g, TAIL_S, H)
         dzT_copy(scopy, g, 1)
-        dz_quant_part(g - 1, PE_COLS, H, dzi_t[g - 1][:, J * PE_COLS:])
-        dzT_quant(g, 0)
-        out0_matmul(g, 0)
-        out0_matmul(g, 1)
-        dz_quant_part(g - 1, 0, PE_COLS, gp_t[:])
+        dz_interleave(scopy, g, TAIL_V, TAIL_S)
+        for v in range(2):
+            nc.vector.quantize_mx(
+                out=tc_t[g, 0][:, P * v:P * (v + 1)].bitcast(E5M2), scales=ts_t[g, 0][:, P * v:P * (v + 1)],
+                in_=dzT_t[g, 0][:, H * v:H * (v + 1)])
+            out0_matmul(g, v)
+        out1_pass(5, 3)
+        dz_quant_part(g - 1, G_PREV, H, dzi_t[g - 1][:, J * G_PREV:])
+        dz_quant_part(g - 1, PE_COLS, G_PREV, gp_t[:, J * PE_COLS:])
+        dz_quant_part(g - 1, 0, PE_COLS, gp_t[:, 0:J * PE_COLS])
         out1_pass(g - 1, 0)
         out1_pass(g - 1, 1)
-        dz_interleave(scopy, g, TAIL_V, TAIL_S)
-        dz_interleave(vcopy, g, G_LAST, TAIL_B)
+        dz_interleave(vcopy, g, G_LAST, TAIL_V)
         dzT_quant(g, 1)
-        out1_pass(g - 1, 2)
-        out0_matmul(g, 2)
         out0_copy(s_scale, g, 0)
         store(g, 0, 1)
+        out0_matmul(g, 2)
         out0_matmul(g, 3, DH_BANK)
+        out1_pass(g - 1, 2)
         out1_pass(g - 1, 3)
-        dz_interleave(vcopy, g, TAIL_B, TAIL_V)
         dz_quant(g)
         for m in range(4):
             out1_pass(g, m)

@@ -30,6 +30,7 @@ H1_SPLIT = 128
 H1_END = 256
 S_FIRST = 384
 G_PREV = 384
+STORES = {3: 0, 5: 3, 6: 5}
 DH_BANK = 3
 FMAX = (2.0 - 2.0 ** -23) * 2.0 ** 127
 
@@ -82,15 +83,22 @@ def tile_mpnnlayer_pb_v_kernel(tc, h1, h_V, mask_attend, W2, b2, W3, b3, z, grad
             nc.sync.dma_start(out=t[:], in_=view)
             return t
 
-        z_t, h1_t = {}, {}
+        rows = new([P, GROUPS * J * H], F32, "rows")
+        h1_all = new([P, GROUPS * J * H], BF16, "h1_all")
+        z_t = {g: rows[:, J * H * g:J * H * (g + 1)] for g in range(GROUPS)}
+        h1_t = {g: h1_all[:, J * H * g:J * H * (g + 1)] for g in range(GROUPS)}
 
-        def load_z(g, lo, hi):
-            if lo == 0:
-                z_t[g] = new([P, J * H], F32, "rows%d" % g)
+        def groups(tile, lo, hi):
+            return tile[:, J * H * lo:J * H * hi].rearrange("p (g c) -> p g c", g=hi - lo)
+
+        def load_z_rows(g, lo, hi):
             nc.sync.dma_start(out=z_t[g][:, H * lo:H * hi], in_=z_v[:, g, H * lo:H * hi])
 
-        def load_h1(g):
-            h1_t[g] = load(h1_v[:, g], J * H, BF16, "h1", GROUPS)
+        def load_z(lo, hi):
+            nc.sync.dma_start(out=groups(rows, lo, hi), in_=z_v[:, lo:hi])
+
+        def load_h1(lo, hi):
+            nc.sync.dma_start(out=groups(h1_all, lo, hi), in_=h1_v[:, lo:hi])
 
         w3_raw, g_raw = {}, {}
         w3_raw[0] = load(w3_v[:, 0], 2 * H, BF16, "w_raw", 2)
@@ -99,19 +107,20 @@ def tile_mpnnlayer_pb_v_kernel(tc, h1, h_V, mask_attend, W2, b2, W3, b3, z, grad
         nc.sync.dma_start(out=mk[0:GROUPS, :], in_=mask_v)
         g_raw[1] = load(grad_v[P:2 * P], H, BF16, "g_first", 2)
         w2_raw = load(w2_v, 4 * H, BF16, "w2_raw", 1)
-        load_z(0, 0, 2)
-        load_h1(1)
-        load_z(0, 2, J)
-        load_h1(0)
-        load_z(1, 0, 2)
-        load_h1(2)
-        load_z(1, 2, J)
-        g_late = new([P, 2 * H], BF16, "g_late")
-        nc.sync.dma_start(out=g_late[:].rearrange("p (t w) -> p t w", t=2), in_=grad_v[2 * P:NODES].rearrange("(t p) w -> p t w", p=P))
-        for g in range(2, GROUPS):
-            if g + 1 < GROUPS:
-                load_h1(g + 1)
-            load_z(g, 0, J)
+        load_z_rows(0, 0, 2)
+        load_h1(1, 2)
+        load_z_rows(0, 2, J)
+        load_h1(0, 1)
+        load_z_rows(1, 0, 2)
+        load_h1(2, 3)
+        load_z_rows(1, 2, J)
+        g_late = load(grad_v[2 * P:NODES].rearrange("(p t) w -> p (t w)", t=2), 2 * H, BF16, "g_late", 1)
+        load_h1(3, 4)
+        load_z(2, 3)
+        load_z(3, 4)
+        for g in range(4, GROUPS, 2):
+            load_h1(g, g + 2)
+            load_z(g, g + 2)
 
         def transpose_stepped(dst, words):
             for u in range(2):
@@ -132,8 +141,11 @@ def tile_mpnnlayer_pb_v_kernel(tc, h1, h_V, mask_attend, W2, b2, W3, b3, z, grad
         def g_first_copy(bv, lo, hi):
             g_copy(g_wide[:].bitcast(F32).rearrange("p (r d u) -> p r d u", d=2, u=2)[:, lo:hi], bv[:, :, lo:hi])
 
-        def g_rest_copy(t, bv):
-            g_copy(g_wide_rest[:].bitcast(F32).rearrange("p (t r d u) -> p t r d u", t=3, d=2, u=2)[:, t], bv)
+        def g_rest_copy(bv):
+            g_copy(g_wide_rest[:].bitcast(F32).rearrange("p (t r d u) -> p t r d u", t=3, d=2, u=2)[:, 0], bv)
+
+        def g_late_copy(t, bv):
+            g_copy(g_wide_rest[:, 8 * P:].bitcast(F32).rearrange("p (r t d u) -> p t r d u", t=2, d=2, u=2)[:, t], bv)
 
         def g_quant(src, first, lo, hi):
             cols = slice(2 * lo, 2 * hi)
@@ -199,11 +211,11 @@ def tile_mpnnlayer_pb_v_kernel(tc, h1, h_V, mask_attend, W2, b2, W3, b3, z, grad
         dh_matmul(0)
         g_first_copy(gb0, 64, P)
         g_quant(g_wide, 0, 64, P)
-        g_rest_copy(0, gb1)
+        g_rest_copy(gb1)
         g_quant(g_wide_rest, P, P, 2 * P)
 
         dz_t, dzi_t, dzc_t, dzs_t, h1i_t, h1c_t, h1s_t = {}, {}, {}, {}, {}, {}, {}
-        tr_t, dzT_t, tc_t, ts_t, o_t, mm_t, acc = {}, {}, {}, {}, {}, {}, {}
+        tr_t, dzT_t, tc_t, ts_t, mm_t, acc = {}, {}, {}, {}, {}, {}
 
         def h1_interleave(g):
             h1i_t[g] = new([P, J * H], BF16, "h1i", 1)
@@ -293,8 +305,6 @@ def tile_mpnnlayer_pb_v_kernel(tc, h1, h_V, mask_attend, W2, b2, W3, b3, z, grad
             nc.vector.quantize_mx(out=tc_t[g, h][:].bitcast(E5M2), scales=ts_t[g, h][:], in_=dzT_t[g, h][:])
 
         def out0_matmul(g, j, tag=None):
-            if j == 0:
-                o_t[g] = new([P, J * H], F32, "rows%d" % g)
             mm_t[g, j] = bank(tag)
             h, v = divmod(j, 2)
             cols = slice(P * v, P * (v + 1))
@@ -312,7 +322,7 @@ def tile_mpnnlayer_pb_v_kernel(tc, h1, h_V, mask_attend, W2, b2, W3, b3, z, grad
             nc.vector.tensor_scalar(out=out, in0=in_, scalar1=0.125, scalar2=None, op0=ALU.mult)
 
         def out0_copy(scale, g, j):
-            scale(o_t[g][:, H * j:H * (j + 1)], mm_t[g, j][:])
+            scale(z_t[g][:, H * j:H * (j + 1)], mm_t[g, j][:])
 
         def out1_pass(g, m):
             if g < 0:
@@ -328,7 +338,10 @@ def tile_mpnnlayer_pb_v_kernel(tc, h1, h_V, mask_attend, W2, b2, W3, b3, z, grad
             )
 
         def store(g, lo, hi):
-            nc.sync.dma_start(out=o_v[:, g, H * lo:H * hi], in_=o_t[g][:, H * lo:H * hi])
+            nc.sync.dma_start(out=o_v[:, g, H * lo:H * hi], in_=z_t[g][:, H * lo:H * hi])
+
+        def store_groups(lo, hi):
+            nc.sync.dma_start(out=o_v[:, lo:hi], in_=groups(rows, lo, hi))
 
         last = GROUPS - 1
 
@@ -399,15 +412,16 @@ def tile_mpnnlayer_pb_v_kernel(tc, h1, h_V, mask_attend, W2, b2, W3, b3, z, grad
             if g == 1:
                 scopy(out=h1i_t[0][:, J * (H - PE_COLS):], in_=h1_bank[:])
             out0_copy(s_scale, g - 1, 3)
-            store(g - 1, 0, J)
+            if g in STORES:
+                store_groups(STORES[g], g)
             dzT_copy(vcopy, g, 0)
             if 1 < g < last - 1:
                 dz_interleave(scopy, g, PE_COLS, S_MID)
             dzT_copy(scopy, g, 1)
             if g == 1:
                 h1_first(H1_END, H - PE_COLS)
-                g_rest_copy(1, gb23[:, 0])
-                g_rest_copy(2, gb23[:, 1])
+                g_late_copy(0, gb23[:, 0])
+                g_late_copy(1, gb23[:, 1])
             if g in (2, 3):
                 g_quant(g_wide_rest, P, P * g, P * (g + 1))
             dh_matmul(g + 1)
@@ -437,14 +451,13 @@ def tile_mpnnlayer_pb_v_kernel(tc, h1, h_V, mask_attend, W2, b2, W3, b3, z, grad
         out1_pass(g - 2, 0)
         out0_copy(s_scale, g - 1, 0)
         out0_copy(s_scale, g - 1, 1)
-        store(g - 1, 0, 2)
         out0_matmul(g - 1, 3)
         dzT_transpose(g, 0)
         out1_pass(g - 2, 1)
         out1_pass(g - 2, 2)
         out0_copy(s_scale, g - 1, 2)
         out0_copy(s_scale, g - 1, 3)
-        store(g - 1, 2, J)
+        store(g - 1, 0, J)
         dz_piece(g, 2, 0)
         dz_piece(g, 3, 0)
         dz_interleave(gcopy, g, 0, G_LAST)
@@ -477,7 +490,6 @@ def tile_mpnnlayer_pb_v_kernel(tc, h1, h_V, mask_attend, W2, b2, W3, b3, z, grad
         dz_interleave(vcopy, g, G_LAST, TAIL_V)
         dzT_quant(g, 1)
         out0_copy(s_scale, g, 0)
-        store(g, 0, 1)
         out0_matmul(g, 2)
         out0_matmul(g, 3, DH_BANK)
         out1_pass(g - 1, 2)
@@ -487,11 +499,13 @@ def tile_mpnnlayer_pb_v_kernel(tc, h1, h_V, mask_attend, W2, b2, W3, b3, z, grad
             out1_pass(g, m)
         for j in range(1, J):
             out0_copy(s_scale if j < 3 else v_scale, g, j)
-            store(g, j, j + 1)
-        o1 = new([P, 4 * H], F32, "rows0")
+            if j % 2 == 1:
+                store(g, j - 1, j + 1)
+        o1 = z_t[0]
         for m in range(4):
             (s_scale if m % 2 == 0 else v_scale)(
                 o1[:, H * m:H * (m + 1)].rearrange("p (q u i) -> p u q i", u=2, i=16),
                 acc[m][:].rearrange("p (u q i) -> p u q i", u=2, i=16),
             )
-            nc.sync.dma_start(out=o1_v[:, m], in_=o1[:, H * m:H * (m + 1)])
+            if m % 2 == 1:
+                nc.sync.dma_start(out=o1_v[:, m - 1:m + 1], in_=o1[:, H * (m - 1):H * (m + 1)].rearrange("p (m w) -> p m w", m=2))

from contextlib import ExitStack

import concourse.mybir as mybir
from concourse.masks import make_identity

F32 = mybir.dt.float32
BF16 = mybir.dt.bfloat16
U32 = mybir.dt.uint32
U8 = mybir.dt.uint8
E4M3 = mybir.dt.float8_e4m3fn_x4
E5M2 = mybir.dt.float8_e5m2_x4
ALU = mybir.AluOpType
ACT = mybir.ActivationFunctionType

P = 128
H = 512
NODES = 512
EDGES = 4096
GROUPS = 8
J = 4
V_FIRST = 64
V_COLS = 0
PE_COLS = 256
S_MID = 256
G_LAST = 128
TAIL_V = 304
V_SECOND = 192
TAIL_S = 352
H1_SPLIT = 128
H1_END = 256
S_FIRST = 384
G_PREV = 384
STORES = {3: 0, 5: 3, 6: 5}
DH_BANK = 3
FMAX = (2.0 - 2.0 ** -23) * 2.0 ** 127

FLOPS = 2 * H * H * (NODES + EDGES + EDGES)
BYTES = 2 * (EDGES * H + EDGES + 2 * H * H + NODES * H) + 4 * (EDGES * H + EDGES * H + H * H)


def tile_mpnnlayer_pb_v_kernel(tc, h1, h_V, mask_attend, W2, b2, W3, b3, z, grad_out, out_0, out_1):
    nc = tc.nc
    h1_v = h1.rearrange("b n k w -> (b n k) w").rearrange("(g p j) w -> p g (j w)", p=P, j=J)
    z_v = z.rearrange("b n k w -> (b n k) w").rearrange("(g p j) w -> p g (j w)", p=P, j=J)
    o_v = out_0.rearrange("b n k w -> (b n k) w").rearrange("(g p j) w -> p g (j w)", p=P, j=J)
    mask_v = mask_attend.rearrange("b n k -> (b n k)").rearrange("(g c) -> g c", g=GROUPS)
    grad_v = grad_out.rearrange("b n w -> (b n) w")
    w2_v = W2.rearrange("(r v) w -> r (v w)", v=4)
    w3_v = W3.rearrange("(b r v) w -> r b (v w)", b=2, v=2)
    o1_v = out_1.rearrange("(m p) w -> p m w", p=P)

    with ExitStack() as ctx:
        ctx.enter_context(tc.manual_schedule())
        sb = ctx.enter_context(tc.tile_pool(name="sb", bufs=1))
        ps = ctx.enter_context(tc.psum_pool(name="ps", bufs=2))

        def new(shape, dtype, tag, bufs=1):
            return sb.tile(shape, dtype, name=tag, tag=tag, bufs=bufs, align_bytes=64)

        ring = [4, 5, 6, 7]

        def bank(k=None, dtype=F32, width=512):
            if k is None:
                k = ring.pop(0)
                ring.append(k)
            return ps.tile([P, width], dtype, name="bank%d" % k, tag="bank%d" % k, bufs=1)

        def blocks(bk):
            return bk[:].rearrange("p (v u r) -> p v u r", u=2, r=P)

        vcopy = nc.vector.tensor_copy
        scopy = nc.scalar.copy

        ident = new([P, P], F32, "ident")
        make_identity(nc, ident[:])
        ident_bf = new([P, P], BF16, "ident_bf")
        make_identity(nc, ident_bf[:])
        mk = new([P, H], BF16, "mk")
        nc.vector.memset(mk[:], 0.0)

        def load(view, width, dtype, tag, bufs):
            t = new([P, width], dtype, tag, bufs)
            nc.sync.dma_start(out=t[:], in_=view)
            return t

        rows = new([P, GROUPS * J * H], F32, "rows")
        h1_all = new([P, GROUPS * J * H], BF16, "h1_all")
        z_t = {g: rows[:, J * H * g:J * H * (g + 1)] for g in range(GROUPS)}
        h1_t = {g: h1_all[:, J * H * g:J * H * (g + 1)] for g in range(GROUPS)}

        def groups(tile, lo, hi):
            return tile[:, J * H * lo:J * H * hi].rearrange("p (g c) -> p g c", g=hi - lo)

        def load_z_rows(g, lo, hi):
            nc.sync.dma_start(out=z_t[g][:, H * lo:H * hi], in_=z_v[:, g, H * lo:H * hi])

        def load_z(lo, hi):
            nc.sync.dma_start(out=groups(rows, lo, hi), in_=z_v[:, lo:hi])

        def load_h1(lo, hi):
            nc.sync.dma_start(out=groups(h1_all, lo, hi), in_=h1_v[:, lo:hi])

        w3_raw, g_raw = {}, {}
        w3_raw[0] = load(w3_v[:, 0], 2 * H, BF16, "w_raw", 2)
        g_raw[0] = load(grad_v[0:P], H, BF16, "g_first", 2)
        w3_raw[1] = load(w3_v[:, 1], 2 * H, BF16, "w_raw", 2)
        nc.sync.dma_start(out=mk[0:GROUPS, :], in_=mask_v)
        g_raw[1] = load(grad_v[P:2 * P], H, BF16, "g_first", 2)
        w2_raw = load(w2_v, 4 * H, BF16, "w2_raw", 1)
        load_z_rows(0, 0, 2)
        load_h1(1, 2)
        load_z_rows(0, 2, J)
        load_h1(0, 1)
        load_z_rows(1, 0, 2)
        load_h1(2, 3)
        load_z_rows(1, 2, J)
        g_late = load(grad_v[2 * P:NODES].rearrange("(p t) w -> p (t w)", t=2), 2 * H, BF16, "g_late", 1)
        load_h1(3, 4)
        load_z(2, 3)
        load_z(3, 4)
        for g in range(4, GROUPS, 2):
            load_h1(g, g + 2)
            load_z(g, g + 2)

        def transpose_stepped(dst, words):
            for u in range(2):
                nc.tensor.transpose(dst[:, u, :], words[:, u:256:2], ident[:])

        def transpose_sorted(dst, words):
            for u in range(2):
                nc.tensor.transpose(dst[:, u, :], words[:, P * u:P * (u + 1)], ident[:])

        g_codes = new([P, 2 * NODES], U32, "g_codes")
        g_scl = new([P, 2 * NODES], U8, "g_scl")
        g_wide = new([P, 8 * P], BF16, "h1i", 1)
        g_wide_rest = new([P, 8 * 3 * P], BF16, "g_wide_rest")

        def g_copy(out, bv):
            scopy(out=out, in_=bv.rearrange("p u r -> p r u").unsqueeze(2).to_broadcast(list(out.shape)))

        def g_first_copy(bv, lo, hi):
            g_copy(g_wide[:].bitcast(F32).rearrange("p (r d u) -> p r d u", d=2, u=2)[:, lo:hi], bv[:, :, lo:hi])

        def g_rest_copy(bv):
            g_copy(g_wide_rest[:].bitcast(F32).rearrange("p (t r d u) -> p t r d u", t=3, d=2, u=2)[:, 0], bv)

        def g_late_copy(t, bv):
            g_copy(g_wide_rest[:, 8 * P:].bitcast(F32).rearrange("p (r t d u) -> p t r d u", t=2, d=2, u=2)[:, t], bv)

        def g_quant(src, first, lo, hi):
            cols = slice(2 * lo, 2 * hi)
            nc.vector.quantize_mx(
                out=g_codes[:, cols].bitcast(E5M2), scales=g_scl[:, cols], in_=src[:, 8 * (lo - first):8 * (hi - first)])

        def w_bank(transposer, raw, tag):
            bv = blocks(bank(tag))
            for v in range(2):
                transposer(bv[:, v], raw[:].bitcast(F32)[:, 256 * v:256 * (v + 1)])
            return bv

        def w_copy(copy, bv):
            dst = new([P, 2 * H], BF16, "w_t", 2)
            copy(out=dst[:].bitcast(F32).rearrange("p (r v u) -> p r v u", v=2, u=2), in_=bv.rearrange("p v u r -> p r v u"))
            return dst

        def w_quant(codes, scl, b, src):
            cols = slice(256 * b, 256 * (b + 1))
            nc.vector.quantize_mx(out=codes[:, cols].bitcast(E4M3), scales=scl[:, cols], in_=src[:])

        def w2_sort(b):
            dst = new([P, 2 * H], BF16, "w2_sorted", 2)
            scopy(
                out=dst[:].rearrange("p (v u q i) -> p v u q i", v=2, u=2, i=16),
                in_=w2_raw[:, 2 * H * b:2 * H * (b + 1)].rearrange("p (v q u i) -> p v u q i", v=2, u=2, i=16),
            )
            return dst

        w3_codes = new([P, H], U32, "w3_codes")
        w3_scl = new([P, H], U8, "w3_scl")
        w2_codes = new([P, H], U32, "w2_codes")
        w2_scl = new([P, H], U8, "w2_scl")
        w3a = w_copy(vcopy, w_bank(transpose_stepped, w3_raw[0], None))
        gb0 = blocks(bank(0))[:, 0]
        transpose_stepped(gb0, g_raw[0][:].bitcast(F32))
        g_first_copy(gb0, 0, 64)
        w3b = w_copy(scopy, w_bank(transpose_stepped, w3_raw[1], None))
        mv = blocks(bank(1))[:, 0]
        transpose_stepped(mv, mk[:].bitcast(F32))
        gb1 = blocks(bank(2))[:, 0]
        transpose_stepped(gb1, g_raw[1][:].bitcast(F32))
        w_quant(w3_codes, w3_scl, 0, w3a)
        g_quant(g_wide, 0, 0, 64)
        m_t = new([P, GROUPS * J], BF16, "m_t")
        vcopy(out=m_t[:].bitcast(F32).rearrange("p (g u) -> p g u", u=2), in_=mv[:, :, 0:GROUPS].rearrange("p u g -> p g u"))
        w_quant(w3_codes, w3_scl, 1, w3b)
        thr = new([P, GROUPS * J], F32, "thr")
        nc.vector.tensor_scalar(out=thr[:], in0=m_t[:], scalar1=-FMAX, scalar2=FMAX, op0=ALU.mult, op1=ALU.add)

        dh_t = {}

        def dh_matmul(g):
            dh_t[g] = bank(DH_BANK)
            cols = slice(P * g, P * (g + 1))
            nc.tensor.matmul_mx(
                out=dh_t[g][:],
                lhsT=g_codes[:, cols].bitcast(E5M2), lhsT_scale=g_scl[:, cols],
                rhs=w3_codes[:].bitcast(E4M3), rhs_scale=w3_scl[:],
                start=True, stop=True,
            )

        dh_matmul(0)
        g_first_copy(gb0, 64, P)
        g_quant(g_wide, 0, 64, P)
        g_rest_copy(gb1)
        g_quant(g_wide_rest, P, P, 2 * P)

        dz_t, dzi_t, dzc_t, dzs_t, h1i_t, h1c_t, h1s_t = {}, {}, {}, {}, {}, {}, {}
        tr_t, dzT_t, tc_t, ts_t, mm_t, acc = {}, {}, {}, {}, {}, {}

        def h1_interleave(g):
            h1i_t[g] = new([P, J * H], BF16, "h1i", 1)
            nc.gpsimd.tensor_scalar(
                out=h1i_t[g][:].rearrange("p (w j) -> p w j", j=J), in0=h1_t[g][:].rearrange("p (j w) -> p w j", j=J),
                scalar1=1.0, scalar2=0.0, op0=ALU.mult, op1=ALU.add)

        def gcopy(out, in_):
            nc.gpsimd.tensor_scalar(out=out, in0=in_, scalar1=1.0, scalar2=0.0, op0=ALU.mult, op1=ALU.add)

        def h1_quant(g):
            h1c_t[g] = new([P, H], U32, "h1c", GROUPS)
            h1s_t[g] = new([P, H], U8, "h1s", GROUPS)
            nc.vector.quantize_mx(out=h1c_t[g][:].bitcast(E4M3), scales=h1s_t[g][:], in_=h1i_t[g][:])

        def dz_piece(g, j, u):
            if g not in dz_t:
                dz_t[g] = new([P, J * H], BF16, "dz", 3)
            nc.vector.scalar_tensor_tensor(
                out=dz_t[g][:, H * j + 256 * u:H * j + 256 * (u + 1)].rearrange("p (q i) -> p q i", i=16),
                in0=z_t[g][:, H * j:H * (j + 1)].rearrange("p (q u i) -> p q u i", u=2, i=16)[:, :, u, :],
                scalar=thr[:, J * g + j:J * g + j + 1],
                in1=dh_t[g][:].rearrange("p (q u i) -> p q u i", u=2, i=16)[:, :, u, :],
                op0=ALU.is_gt, op1=ALU.mult,
            )

        def dz_compute(g, h):
            for j in (2 * h, 2 * h + 1):
                for u in range(2):
                    dz_piece(g, j, u)

        def dz_interleave(copy, g, lo, hi):
            if g not in dzi_t:
                dzi_t[g] = new([P, J * H], BF16, "dzi", 2)
            if hi <= lo:
                return
            out = dzi_t[g][:].rearrange("p (w j) -> p w j", j=J)[:, lo:hi, :]
            in_ = dz_t[g][:].rearrange("p (j w) -> p w j", j=J)[:, lo:hi, :]
            if copy is gcopy:
                copy(out=out, in_=in_)
            else:
                copy(out=out.rearrange("p (c i) j -> p c j i", i=4), in_=in_.rearrange("p (c i) j -> p c j i", i=4))

        pe_t = {}

        def pe_rows(src, lo, dst, c):
            nc.tensor.matmul(
                dst[:, J * c:J * (c + P)].rearrange("p (c i j) -> p c j i", i=8, j=J), lhsT=ident_bf[:],
                rhs=src[:].rearrange("p (j w) -> p j w", j=J)[:, :, lo + c:lo + c + P].rearrange("p j (c i) -> p c j i", i=8),
                start=True, stop=True)

        def pe_interleave(g):
            pe_t[g] = bank(None, BF16, J * PE_COLS)
            for c in range(0, PE_COLS, P):
                pe_rows(dz_t[g], 0, pe_t[g], c)

        def pe_copy(g):
            if g not in dzi_t:
                dzi_t[g] = new([P, J * H], BF16, "dzi", 2)
            scopy(out=dzi_t[g][:, 0:J * PE_COLS], in_=pe_t[g][:])

        def dz_quant_part(g, lo, hi, src):
            if g not in dzc_t:
                dzc_t[g] = new([P, H], U32, "dzc", GROUPS)
                dzs_t[g] = new([P, H], U8, "dzs", GROUPS)
            nc.vector.quantize_mx(out=dzc_t[g][:, lo:hi].bitcast(E5M2), scales=dzs_t[g][:, lo:hi], in_=src)

        def dz_quant(g):
            dz_quant_part(g, 0, H, dzi_t[g][:])

        def dzT_transpose(g, h, tag=None):
            tr_t[g, h] = blocks(bank(tag))
            for v in range(2):
                j = 2 * h + v
                transpose_sorted(tr_t[g, h][:, v], dz_t[g][:].bitcast(F32)[:, 256 * j:256 * (j + 1)])

        def dzT_copy(copy, g, h):
            dzT_t[g, h] = new([P, 2 * P * 4], BF16, "dzT", 3)
            copy(
                out=dzT_t[g, h][:].bitcast(F32).rearrange("p (v r u) -> p v r u", r=P, u=2),
                in_=tr_t[g, h].rearrange("p v u r -> p v r u"),
            )

        def dzT_quant(g, h):
            tc_t[g, h] = new([P, 2 * P], U32, "tcod", 3)
            ts_t[g, h] = new([P, 2 * P], U8, "tscl", 3)
            nc.vector.quantize_mx(out=tc_t[g, h][:].bitcast(E5M2), scales=ts_t[g, h][:], in_=dzT_t[g, h][:])

        def out0_matmul(g, j, tag=None):
            mm_t[g, j] = bank(tag)
            h, v = divmod(j, 2)
            cols = slice(P * v, P * (v + 1))
            nc.tensor.matmul_mx(
                out=mm_t[g, j][:],
                lhsT=tc_t[g, h][:, cols].bitcast(E5M2), lhsT_scale=ts_t[g, h][:, cols],
                rhs=w2_codes[:].bitcast(E4M3), rhs_scale=w2_scl[:],
                start=True, stop=True,
            )

        def s_scale(out, in_):
            nc.scalar.activation(out=out, in_=in_, func=ACT.Copy, scale=0.125)

        def v_scale(out, in_):
            nc.vector.tensor_scalar(out=out, in0=in_, scalar1=0.125, scalar2=None, op0=ALU.mult)

        def out0_copy(scale, g, j):
            scale(z_t[g][:, H * j:H * (j + 1)], mm_t[g, j][:])

        def out1_pass(g, m):
            if g < 0:
                return
            if g == 0:
                acc[m] = bank(m if m < 3 else ring.pop(0))
            cols = slice(P * m, P * (m + 1))
            nc.tensor.matmul_mx(
                out=acc[m][:],
                lhsT=h1c_t[g][:, cols].bitcast(E4M3), lhsT_scale=h1s_t[g][:, cols],
                rhs=dzc_t[g][:].bitcast(E5M2), rhs_scale=dzs_t[g][:],
                start=(g == 0), stop=(g == GROUPS - 1),
            )

        def store(g, lo, hi):
            nc.sync.dma_start(out=o_v[:, g, H * lo:H * hi], in_=z_t[g][:, H * lo:H * hi])

        def store_groups(lo, hi):
            nc.sync.dma_start(out=o_v[:, lo:hi], in_=groups(rows, lo, hi))

        last = GROUPS - 1

        w2_sorted = [w2_sort(b) for b in range(2)]
        h1_interleave(1)
        w2_banks = [w_bank(transpose_sorted, w2_sorted[b], (1, 0)[b]) for b in range(2)]
        dz_compute(0, 0)
        dzT_transpose(0, 0)
        w2_t = new([P, 4 * H], BF16, "w2_t")
        for b in range(2):
            scopy(
                out=w2_t[:].bitcast(F32).rearrange("p (r b v u) -> p r b v u", b=2, v=2, u=2)[:, :, b],
                in_=w2_banks[b].rearrange("p v u r -> p r v u"),
            )
        dz_compute(0, 1)
        dzT_transpose(0, 1)
        dh_matmul(1)
        h1i_t[0] = new([P, J * H], BF16, "h1i_first")

        def h1_first(lo, hi):
            if hi <= lo:
                return
            scopy(
                out=h1i_t[0][:].rearrange("p (c i j) -> p c j i", i=4, j=J)[:, lo // 4:hi // 4],
                in_=h1_t[0][:].rearrange("p (j c i) -> p c j i", i=4, j=J)[:, lo // 4:hi // 4],
            )

        dzT_copy(vcopy, 0, 0)
        h1_first(0, H1_SPLIT)
        dzT_copy(scopy, 0, 1)
        nc.vector.quantize_mx(out=w2_codes[:].bitcast(E4M3), scales=w2_scl[:], in_=w2_t[:])
        pe_interleave(0)
        dzT_quant(0, 0)
        out0_matmul(0, 0)
        out0_matmul(0, 1)
        dz_interleave(vcopy, 0, H - V_FIRST, H)
        h1_first(H1_SPLIT, H1_END)
        dz_interleave(scopy, 0, PE_COLS, S_FIRST)
        h1_quant(1)
        dzT_quant(0, 1)

        for g in range(1, last):
            h1_interleave(g + 1)
            dz_compute(g, 0)
            out0_matmul(g - 1, 2)
            out1_pass(g - 2, 0)
            out1_pass(g - 2, 1)
            if g == 1:
                h1_bank = bank(0, BF16, J * PE_COLS)
                pe_rows(h1_t[0], H - PE_COLS, h1_bank, 0)
            pe_copy(g - 1)
            dzT_transpose(g, 0)
            if g == 1:
                pe_rows(h1_t[0], H - PE_COLS, h1_bank, P)
            out0_copy(s_scale, g - 1, 0)
            out0_matmul(g - 1, 3)
            out1_pass(g - 2, 2)
            out0_copy(s_scale, g - 1, 1)
            if g == 1:
                dz_interleave(scopy, 0, S_FIRST, H - V_FIRST)
            dz_compute(g, 1)
            dzT_transpose(g, 1)
            if g == 1:
                gb23 = blocks(bank(1))
                for v in range(2):
                    transpose_stepped(gb23[:, v], g_late[:].bitcast(F32)[:, 256 * v:256 * (v + 1)])
            out0_copy(s_scale, g - 1, 2)
            if g == 1:
                scopy(out=h1i_t[0][:, J * (H - PE_COLS):], in_=h1_bank[:])
            out0_copy(s_scale, g - 1, 3)
            if g in STORES:
                store_groups(STORES[g], g)
            dzT_copy(vcopy, g, 0)
            if 1 < g < last - 1:
                dz_interleave(scopy, g, PE_COLS, S_MID)
            dzT_copy(scopy, g, 1)
            if g == 1:
                h1_first(H1_END, H - PE_COLS)
                g_late_copy(0, gb23[:, 0])
                g_late_copy(1, gb23[:, 1])
            if g in (2, 3):
                g_quant(g_wide_rest, P, P * g, P * (g + 1))
            dh_matmul(g + 1)
            dz_quant(g - 1)
            if g < last - 1:
                pe_interleave(g)
            else:
                for k in range(3):
                    out1_pass(k, 3)
            dzT_quant(g, 0)
            out0_matmul(g, 0)
            out0_matmul(g, 1)
            if g == last - 1:
                out1_pass(3, 3)
            dz_interleave(vcopy, g, H - (V_SECOND if g == 1 else V_COLS), H)
            dz_interleave(scopy, g, {1: PE_COLS, last - 1: G_PREV}.get(g, S_MID), H - (V_SECOND if g == 1 else V_COLS))
            if g == 1:
                h1_quant(0)
            h1_quant(g + 1)
            dzT_quant(g, 1)

        g = last
        gp_t = new([P, J * G_PREV], BF16, "h1i", 1)
        gcopy(gp_t[:].rearrange("p (w j) -> p w j", j=J), dz_t[g - 1][:].rearrange("p (j w) -> p w j", j=J)[:, 0:G_PREV])
        dz_compute(g, 0)
        out0_matmul(g - 1, 2)
        out1_pass(g - 2, 0)
        out0_copy(s_scale, g - 1, 0)
        out0_copy(s_scale, g - 1, 1)
        out0_matmul(g - 1, 3)
        dzT_transpose(g, 0)
        out1_pass(g - 2, 1)
        out1_pass(g - 2, 2)
        out0_copy(s_scale, g - 1, 2)
        out0_copy(s_scale, g - 1, 3)
        store(g - 1, 0, J)
        dz_piece(g, 2, 0)
        dz_piece(g, 3, 0)
        dz_interleave(gcopy, g, 0, G_LAST)
        dz_piece(g, 2, 1)
        dz_piece(g, 3, 1)
        dzT_transpose(g, 1, DH_BANK)
        out1_pass(4, 3)
        dzT_t[g, 0] = new([P, 2 * P * 4], BF16, "dzT", 3)
        tc_t[g, 0] = new([P, 2 * P], U32, "tcod", 3)
        ts_t[g, 0] = new([P, 2 * P], U8, "tscl", 3)
        for v in range(2):
            vcopy(
                out=dzT_t[g, 0][:, H * v:H * (v + 1)].bitcast(F32).rearrange("p (r u) -> p r u", u=2),
                in_=tr_t[g, 0][:, v].rearrange("p u r -> p r u"),
            )
        dz_interleave(scopy, g, TAIL_S, H)
        dzT_copy(scopy, g, 1)
        dz_interleave(scopy, g, TAIL_V, TAIL_S)
        for v in range(2):
            nc.vector.quantize_mx(
                out=tc_t[g, 0][:, P * v:P * (v + 1)].bitcast(E5M2), scales=ts_t[g, 0][:, P * v:P * (v + 1)],
                in_=dzT_t[g, 0][:, H * v:H * (v + 1)])
            out0_matmul(g, v)
        out1_pass(5, 3)
        dz_quant_part(g - 1, G_PREV, H, dzi_t[g - 1][:, J * G_PREV:])
        dz_quant_part(g - 1, PE_COLS, G_PREV, gp_t[:, J * PE_COLS:])
        dz_quant_part(g - 1, 0, PE_COLS, gp_t[:, 0:J * PE_COLS])
        out1_pass(g - 1, 0)
        out1_pass(g - 1, 1)
        dz_interleave(vcopy, g, G_LAST, TAIL_V)
        dzT_quant(g, 1)
        out0_copy(s_scale, g, 0)
        out0_matmul(g, 2)
        out0_matmul(g, 3, DH_BANK)
        out1_pass(g - 1, 2)
        out1_pass(g - 1, 3)
        dz_quant(g)
        for m in range(4):
            out1_pass(g, m)
        for j in range(1, J):
            out0_copy(s_scale if j < 3 else v_scale, g, j)
            if j % 2 == 1:
                store(g, j - 1, j + 1)
        o1 = z_t[0]
        for m in range(4):
            (s_scale if m % 2 == 0 else v_scale)(
                o1[:, H * m:H * (m + 1)].rearrange("p (q u i) -> p u q i", u=2, i=16),
                acc[m][:].rearrange("p (u q i) -> p u q i", u=2, i=16),
            )
            if m % 2 == 1:
                nc.sync.dma_start(out=o1_v[:, m - 1:m + 1], in_=o1[:, H * (m - 1):H * (m + 1)].rearrange("p (m w) -> p m w", m=2))
